import numpy as np
import ml_dtypes


def mxq(x, axis, fmt="e4m3"):
    dtype, down = {"e4m3": (ml_dtypes.float8_e4m3fn, 7), "e5m2": (ml_dtypes.float8_e5m2, 14)}[fmt]
    v = np.moveaxis(np.asarray(x, np.float32).astype(ml_dtypes.bfloat16).astype(np.float64), axis, -1)
    blocks = v.reshape(v.shape[:-1] + (-1, 32))
    amax = np.abs(blocks).max(-1, keepdims=True)
    byte = np.maximum(np.where(amax > 0, np.frexp(amax)[1] - 1 + 127, 0) - down, 1)
    scale = np.exp2(byte - 127.0)
    codes = (blocks / scale).astype(np.float32).astype(dtype).astype(np.float64)
    return np.moveaxis((codes * scale).reshape(v.shape), -1, axis)


WIDE = False


def mx_kscale(k):
    if not WIDE:
        return np.ones(k)
    levels = np.array([10, -10, 5, -5, 0])
    a = np.random.permutation(np.resize(levels, k // 512 * 4)).reshape(k // 512, 4)
    idx = np.arange(k)
    return np.exp2(a[idx // 512, idx % 128 // 32])


BF16 = ml_dtypes.bfloat16


def bf(x):
    return np.asarray(x, np.float32).astype(BF16)


def f64(x):
    return np.asarray(x).astype(np.float64)


E2M1 = np.array([0.0, 0.5, 1.0, 1.5, 2.0, 3.0, 4.0, 6.0, -0.0, -0.5, -1.0, -1.5, -2.0, -3.0, -4.0, -6.0])


def pack_weight(w, fmt):
    k, n = w.shape
    w = f64(bf(w)).reshape(k // 32, 32, n)
    amax = np.abs(w).max(1)
    if fmt == "e4m3":
        byte = np.frexp(amax)[1] - 1 + 127 - 7
    else:
        mant, ex = np.frexp(amax / 6.0)
        byte = np.where(mant > 0.5, ex, ex - 1) + 127
    byte = np.clip(np.where(amax > 0, byte, 1), 1, 254)
    scaled = (w * np.exp2(127.0 - byte)[:, None, :]).reshape(k, n).astype(np.float32)
    by_word = np.ascontiguousarray(scaled.reshape(k // 512, 128, 4, n).transpose(0, 1, 3, 2))
    if fmt == "e4m3":
        words = by_word.astype(ml_dtypes.float8_e4m3fn).view(np.uint8)
    else:
        c = by_word.astype(ml_dtypes.float4_e2m1fn).view(np.uint8) & 0xF
        words = c[..., 0::2] | (c[..., 1::2] << 4)
    return np.ascontiguousarray(words), np.ascontiguousarray(byte.astype(np.uint8).reshape(k // 512, 16, n))


def unpack_weight(words, scales, fmt):
    g, p, n, _ = words.shape
    if fmt == "e4m3":
        vals = np.ascontiguousarray(words).view(ml_dtypes.float8_e4m3fn).astype(np.float64)
    else:
        nib = np.empty((g, p, n, 4), np.uint8)
        nib[..., 0::2] = words & 0xF
        nib[..., 1::2] = words >> 4
        vals = E2M1[nib]
    vals = vals * np.repeat(np.exp2(scales.astype(np.float64) - 127.0), 8, axis=1)[..., None]
    return vals.transpose(0, 1, 3, 2).reshape(g * 512, n)


B, IDIM, HDIM, ODIM, S, DEPTH, NACT, NTOP = 1024, 512, 1024, 512, 128, 32, 3, 2
FMT = "e4m3"


def sigmoid(v):
    return 1.0 / (1.0 + np.exp(-v))


def setup_inputs():
    s = mx_kscale(HDIM)
    h = bf(sigmoid(np.random.standard_normal((B, HDIM)) * 1.3) * s)
    stack = bf(np.random.standard_normal((B, DEPTH, S)))
    Wa_words, Wa_scales = pack_weight((np.random.standard_normal((NACT * S, HDIM)) * 3.0 / np.sqrt(HDIM) / s).T, FMT)
    ba = bf(np.random.standard_normal(NACT * S) * 0.5)
    Ws_words, Ws_scales = pack_weight((np.random.standard_normal((S, HDIM)) * 2.0 / np.sqrt(HDIM) / s).T, FMT)
    bs = bf(np.random.standard_normal(S))
    Wo_words, Wo_scales = pack_weight((np.random.standard_normal((ODIM, HDIM)) * 2.0 / np.sqrt(HDIM) / s).T, FMT)
    bo = bf(np.random.standard_normal(ODIM) * 0.3)
    return {"h": h,
            "stack": stack,
            "Wa_words": Wa_words,
            "Wa_scales": Wa_scales,
            "ba": ba,
            "Ws_words": Ws_words,
            "Ws_scales": Ws_scales,
            "bs": bs,
            "Wo_words": Wo_words,
            "Wo_scales": Wo_scales,
            "bo": bo}


def reference(h, stack, Wa_words, Wa_scales, ba, Ws_words, Ws_scales, bs, Wo_words, Wo_scales, bo):
    st = f64(stack)
    hq = mxq(f64(h), 1, "e4m3")
    logits = ((hq @ unpack_weight(Wa_words, Wa_scales, FMT)) + f64(ba)).reshape(-1, NACT, S)
    e = np.exp(logits - logits.max(axis=1, keepdims=True))
    act = e / e.sum(axis=1, keepdims=True)
    top = sigmoid((hq @ unpack_weight(Ws_words, Ws_scales, FMT)) + f64(bs))[:, None, :]
    push = np.concatenate([top, st[:, :-1]], axis=1)
    empty = np.full((st.shape[0], 1, S), -1.0)
    pop = np.concatenate([st[:, 1:], empty], axis=1)
    new_stack = (push * act[:, 0][:, None, :]
                 + pop * act[:, 1][:, None, :]
                 + st * act[:, 2][:, None, :])
    out = (hq @ unpack_weight(Wo_words, Wo_scales, FMT)) + f64(bo)
    return out, new_stack

@@ -1,0 +1,215 @@
+from contextlib import ExitStack
+
+import concourse.mybir as mybir
+from concourse.masks import make_identity
+
+F32 = mybir.dt.float32
+BF16 = mybir.dt.bfloat16
+I32 = mybir.dt.int32
+U32 = mybir.dt.uint32
+U8 = mybir.dt.uint8
+FP8X4 = mybir.dt.float8_e4m3fn_x4
+FUNC = mybir.ActivationFunctionType
+ALU = mybir.AluOpType
+
+P = 128
+BATCH = 1024
+K = 1024
+K_PASS = 512
+PASSES = K // K_PASS
+S = 128
+DEPTH = 32
+N_OUT = 512
+N_GATES = 4 * S
+B_TILES = BATCH // P
+PUSH, POP, KEEP = 0, 1, 2
+ROWS = 8
+GROUPS = DEPTH // ROWS
+BANK_ROWS = 4
+
+FLOPS = 2 * BATCH * K * (N_GATES + N_OUT)
+
+
+def tile_stackrnn_pb_kernel(
+    tc, h, stack, Wa_words, Wa_scales, ba, Ws_words, Ws_scales, bs, Wo_words, Wo_scales, bo, out_0, out_1
+):
+    nc = tc.nc
+    with ExitStack() as ctx:
+        const = ctx.enter_context(tc.tile_pool(name="const", bufs=1))
+        loads = ctx.enter_context(tc.tile_pool(name="loads", bufs=4))
+        quant = ctx.enter_context(tc.tile_pool(name="quant", bufs=2))
+        soft = ctx.enter_context(tc.tile_pool(name="soft", bufs=2))
+        gate_pool = ctx.enter_context(tc.tile_pool(name="gates", bufs=3))
+        term_pool = ctx.enter_context(tc.tile_pool(name="terms", bufs=2))
+        stage = ctx.enter_context(tc.tile_pool(name="stage", bufs=4))
+        psum = ctx.enter_context(tc.psum_pool(name="psum", bufs=1))
+
+        ident_f32 = const.tile([P, P], F32, name="ident_f32")
+        make_identity(nc, ident_f32[:])
+        ident_bf16 = const.tile([P, P], BF16, name="ident_bf16")
+        make_identity(nc, ident_bf16[:])
+
+        def load_tile(t):
+            rows = slice(t * P, (t + 1) * P)
+            h_sb = loads.tile([P, K], BF16, name="h_sb")
+            nc.sync.dma_start(out=h_sb[:], in_=h[rows, :])
+            x_sb = loads.tile([P, DEPTH, S], BF16, name="x_sb")
+            nc.sync.dma_start(out=x_sb[:], in_=stack[rows, :, :])
+            return h_sb, x_sb
+
+        w_codes = const.tile([P, PASSES, N_GATES + N_OUT], U32, name="w_codes", align_bytes=64)
+        w_scales = const.tile([P, PASSES, N_GATES + N_OUT], U8, name="w_scales", align_bytes=64)
+        nc.vector.memset(w_scales[:].bitcast(I32), 0)
+        bias_rows = const.tile([P, P], BF16, name="bias_rows")
+        nc.vector.memset(bias_rows[:].bitcast(I32), 0)
+
+        first_loads = load_tile(0)
+        weights = ((Wa_words, Wa_scales, 0, 3 * S), (Ws_words, Ws_scales, 3 * S, S), (Wo_words, Wo_scales, N_GATES, N_OUT))
+        for words, scales, first, width in weights:
+            nc.sync.dma_start(
+                out=w_codes[:, :, first : first + width].bitcast(I32),
+                in_=words.rearrange("g p n t -> p g (n t)").bitcast(I32),
+            )
+        for words, scales, first, width in weights:
+            for quad in range(4):
+                nc.sync.dma_start(
+                    out=w_scales[32 * quad : 32 * quad + 4, :, first : first + width].bitcast(I32),
+                    in_=scales[:, 4 * quad : 4 * quad + 4, :].rearrange("g r n -> r g n").bitcast(I32),
+                )
+
+        nc.sync.dma_start(out=bias_rows[0:3, :], in_=ba.rearrange("(a s) -> a s", a=3))
+        nc.sync.dma_start(out=bias_rows[3:4, :], in_=bs.rearrange("(a s) -> a s", a=1))
+        bias_ps = psum.tile([P, P], BF16, name="bias_ps", tag="hT")
+        nc.tensor.transpose(bias_ps[:], bias_rows[:], ident_bf16[:])
+        bias_col = const.tile([P, 4], F32, name="bias_col")
+        nc.vector.tensor_copy(out=bias_col[:], in_=bias_ps[:, 0:4])
+        half_bs = const.tile([P, 1], F32, name="half_bs")
+        nc.vector.tensor_scalar_mul(out=half_bs[:], in0=bias_col[:, 3:4], scalar1=0.5)
+        bo_all = const.tile([P, N_OUT], BF16, name="bo_all")
+        nc.sync.dma_start(out=bo_all[:], in_=bo.partition_broadcast(P))
+
+        def gates_and_out(t, h_sb):
+            rows = slice(t * P, (t + 1) * P)
+            h_words = h_sb[:].bitcast(F32)
+            hT = psum.tile([P, PASSES, 2, P], F32, name="hT", tag="hT")
+            for g in range(PASSES):
+                for u in range(2):
+                    nc.tensor.transpose(hT[:, g, u, :], h_words[:, 256 * g + u : 256 * (g + 1) : 2], ident_f32[:])
+            grouped = quant.tile([P, PASSES, P, 4], BF16, name="grouped", align_bytes=64)
+            nc.scalar.copy(out=grouped[:].bitcast(F32), in_=hT[:].rearrange("p g u b -> p g b u"))
+            h_codes = quant.tile([P, PASSES, P], U32, name="h_codes", align_bytes=64)
+            h_scales = quant.tile([P, PASSES, P], U8, name="h_scales", align_bytes=64)
+            nc.vector.quantize_mx(
+                out=h_codes[:].rearrange("p g b -> p (g b)").bitcast(FP8X4),
+                scales=h_scales[:].rearrange("p g b -> p (g b)"),
+                in_=grouped[:].rearrange("p g b t -> p (g b t)"),
+            )
+
+            logits = psum.tile([P, 4, P], F32, name="logits", tag="logits")
+            for j in range(4):
+                cols = slice(j * S, (j + 1) * S)
+                for g in range(PASSES):
+                    nc.tensor.matmul_mx(
+                        out=logits[:, j, :],
+                        lhsT=w_codes[:, g, cols].bitcast(FP8X4),
+                        lhsT_scale=w_scales[:, g, cols],
+                        rhs=h_codes[:, g, :].bitcast(FP8X4),
+                        rhs_scale=h_scales[:, g, :],
+                        start=(g == 0),
+                        stop=(g == PASSES - 1),
+                    )
+            out_ps = psum.tile([P, N_OUT], F32, name="out_ps", tag="out_ps")
+            for g in range(PASSES):
+                nc.tensor.matmul_mx(
+                    out=out_ps[:],
+                    lhsT=h_codes[:, g, :].bitcast(FP8X4),
+                    lhsT_scale=h_scales[:, g, :],
+                    rhs=w_codes[:, g, N_GATES:].bitcast(FP8X4),
+                    rhs_scale=w_scales[:, g, N_GATES:],
+                    start=(g == 0),
+                    stop=(g == PASSES - 1),
+                )
+            out_sb = stage.tile([P, N_OUT], F32, name="out_sb")
+            nc.vector.tensor_add(out=out_sb[:], in0=out_ps[:], in1=bo_all[:])
+            nc.sync.dma_start(out=out_0[rows, :], in_=out_sb[:])
+
+            logit_sb = soft.tile([P, 3, P], F32, name="logit_sb")
+            for a in range(3):
+                nc.scalar.activation(
+                    out=logit_sb[:, a, :], in_=logits[:, a, :], func=FUNC.Identity, bias=bias_col[:, a : a + 1]
+                )
+            tanh_half = soft.tile([P, P], F32, name="tanh_half")
+            nc.scalar.activation(out=tanh_half[:], in_=logits[:, 3, :], func=FUNC.Tanh, bias=half_bs[:], scale=0.5)
+            over_actions = [P, 3, P]
+            peak = soft.tile([P, P], F32, name="peak")
+            nc.vector.tensor_max(out=peak[:], in0=logit_sb[:, 0, :], in1=logit_sb[:, 1, :])
+            nc.vector.tensor_max(out=peak[:], in0=peak[:], in1=logit_sb[:, 2, :])
+            nc.vector.tensor_sub(out=logit_sb[:], in0=logit_sb[:], in1=peak[:].unsqueeze(1).to_broadcast(over_actions))
+            expo = soft.tile([P, 3, P], F32, name="expo")
+            nc.scalar.activation(out=expo[:], in_=logit_sb[:], func=FUNC.Exp)
+            total = soft.tile([P, P], F32, name="total")
+            nc.vector.tensor_add(out=total[:], in0=expo[:, 0, :], in1=expo[:, 1, :])
+            nc.vector.tensor_add(out=total[:], in0=total[:], in1=expo[:, 2, :])
+            inverse = soft.tile([P, P], F32, name="inverse")
+            nc.vector.reciprocal(out=inverse[:], in_=total[:])
+            gates = gate_pool.tile([P, 3, P], F32, name="gates")
+            nc.vector.tensor_mul(out=gates[:], in0=expo[:], in1=inverse[:].unsqueeze(1).to_broadcast(over_actions))
+
+            top = soft.tile([P, P], F32, name="top")
+            nc.vector.tensor_scalar(out=top[:], in0=tanh_half[:], scalar1=0.5, scalar2=0.5, op0=ALU.mult, op1=ALU.add)
+            edges = gate_pool.tile([P, 2, P], F32, name="edges")
+            nc.vector.tensor_mul(out=edges[:, 0, :], in0=gates[:, PUSH, :], in1=top[:])
+            nc.vector.tensor_scalar_mul(out=edges[:, 1, :], in0=gates[:, POP, :], scalar1=-1.0)
+            return gates, edges
+
+        def multiply_group(t, j, x_sb, gates, terms):
+            first = j * ROWS
+            xT = psum.tile([P, ROWS, P], BF16, name="xT", tag="xT", bufs=2)
+            for i in range(ROWS):
+                nc.tensor.transpose(xT[:, i, :], x_sb[:, first + i, :], ident_bf16[:])
+            shape = [P, 3, ROWS, P]
+            product = terms[:, :, first : first + ROWS, :]
+            gate_view = gates[:].unsqueeze(2).to_broadcast(shape)
+            if (t * GROUPS + j) % 3 == 1:
+                xT_sb = stage.tile([P, ROWS, P], BF16, name="xT_sb")
+                nc.scalar.copy(out=xT_sb[:], in_=xT[:])
+                nc.gpsimd.tensor_tensor(out=product, in0=xT_sb[:].unsqueeze(1).to_broadcast(shape), in1=gate_view, op=ALU.mult)
+            else:
+                nc.vector.tensor_tensor(out=product, in0=xT[:].unsqueeze(1).to_broadcast(shape), in1=gate_view, op=ALU.mult)
+
+        def add_group(t, j, terms, edges):
+            rows = slice(t * P, (t + 1) * P)
+            new_sb = stage.tile([P, ROWS, S], F32, name="new_sb")
+            for part in range(ROWS // BANK_ROWS):
+                new_ps = psum.tile([P, BANK_ROWS, S], F32, name="new_ps", tag="new_ps", bufs=3)
+                for i in range(BANK_ROWS):
+                    d = j * ROWS + part * BANK_ROWS + i
+                    pushed = edges[:, 0, :] if d == 0 else terms[:, PUSH, d - 1, :]
+                    popped = edges[:, 1, :] if d == DEPTH - 1 else terms[:, POP, d + 1, :]
+                    summands = (pushed, terms[:, KEEP, d, :], popped)
+                    for n, term in enumerate(summands):
+                        nc.tensor.matmul(
+                            out=new_ps[:, i, :],
+                            lhsT=term,
+                            rhs=ident_f32[:],
+                            is_transpose=True,
+                            start=(n == 0),
+                            stop=(n == len(summands) - 1),
+                        )
+                nc.scalar.copy(out=new_sb[:, part * BANK_ROWS : (part + 1) * BANK_ROWS, :], in_=new_ps[:])
+            nc.scalar.dma_start(out=out_1[rows, j * ROWS : (j + 1) * ROWS, :], in_=new_sb[:])
+
+        h_sb, x_sb = first_loads
+        gates, edges = gates_and_out(0, h_sb)
+        for t in range(B_TILES):
+            if t + 1 < B_TILES:
+                next_h, next_x = load_tile(t + 1)
+                next_gates, next_edges = gates_and_out(t + 1, next_h)
+            terms = term_pool.tile([P, 3, DEPTH, P], F32, name="terms")
+            for j in range(GROUPS):
+                multiply_group(t, j, x_sb, gates, terms)
+                if j > 0:
+                    add_group(t, j - 1, terms, edges)
+            add_group(t, GROUPS - 1, terms, edges)
+            if t + 1 < B_TILES:
+                x_sb, gates, edges = next_x, next_gates, next_edges

@@ -23,9 +23,11 @@ N_OUT = 512
 N_GATES = 4 * S
 B_TILES = BATCH // P
 PUSH, POP, KEEP = 0, 1, 2
-ROWS = 8
+ROWS = 4
 GROUPS = DEPTH // ROWS
-BANK_ROWS = 4
+VECTOR_GROUPS = 5
+PAIR = 2 * ROWS
+PAIRS = DEPTH // PAIR
 
 FLOPS = 2 * BATCH * K * (N_GATES + N_OUT)
 
@@ -63,7 +65,7 @@ def tile_stackrnn_pb_kernel(
         bias_rows = const.tile([P, P], BF16, name="bias_rows")
         nc.vector.memset(bias_rows[:].bitcast(I32), 0)
 
-        first_loads = load_tile(0)
+        tiles_in = [load_tile(0)]
         weights = ((Wa_words, Wa_scales, 0, 3 * S), (Ws_words, Ws_scales, 3 * S, S), (Wo_words, Wo_scales, N_GATES, N_OUT))
         for words, scales, first, width in weights:
             nc.sync.dma_start(
@@ -88,8 +90,8 @@ def tile_stackrnn_pb_kernel(
         bo_all = const.tile([P, N_OUT], BF16, name="bo_all")
         nc.sync.dma_start(out=bo_all[:], in_=bo.partition_broadcast(P))
 
-        def gates_and_out(t, h_sb):
-            rows = slice(t * P, (t + 1) * P)
+        def quantise_h(t):
+            h_sb = tiles_in[t][0]
             h_words = h_sb[:].bitcast(F32)
             hT = psum.tile([P, PASSES, 2, P], F32, name="hT", tag="hT")
             for g in range(PASSES):
@@ -104,7 +106,10 @@ def tile_stackrnn_pb_kernel(
                 scales=h_scales[:].rearrange("p g b -> p (g b)"),
                 in_=grouped[:].rearrange("p g b t -> p (g b t)"),
             )
+            return h_codes, h_scales
 
+        def matmuls(t, h_codes, h_scales):
+            rows = slice(t * P, (t + 1) * P)
             logits = psum.tile([P, 4, P], F32, name="logits", tag="logits")
             for j in range(4):
                 cols = slice(j * S, (j + 1) * S)
@@ -132,7 +137,11 @@ def tile_stackrnn_pb_kernel(
             out_sb = stage.tile([P, N_OUT], F32, name="out_sb")
             nc.vector.tensor_add(out=out_sb[:], in0=out_ps[:], in1=bo_all[:])
             nc.sync.dma_start(out=out_0[rows, :], in_=out_sb[:])
+            return logits
 
+        over_actions = [P, 3, P]
+
+        def exponentials(logits):
             logit_sb = soft.tile([P, 3, P], F32, name="logit_sb")
             for a in range(3):
                 nc.scalar.activation(
@@ -140,13 +149,15 @@ def tile_stackrnn_pb_kernel(
                 )
             tanh_half = soft.tile([P, P], F32, name="tanh_half")
             nc.scalar.activation(out=tanh_half[:], in_=logits[:, 3, :], func=FUNC.Tanh, bias=half_bs[:], scale=0.5)
-            over_actions = [P, 3, P]
             peak = soft.tile([P, P], F32, name="peak")
             nc.vector.tensor_max(out=peak[:], in0=logit_sb[:, 0, :], in1=logit_sb[:, 1, :])
             nc.vector.tensor_max(out=peak[:], in0=peak[:], in1=logit_sb[:, 2, :])
             nc.vector.tensor_sub(out=logit_sb[:], in0=logit_sb[:], in1=peak[:].unsqueeze(1).to_broadcast(over_actions))
             expo = soft.tile([P, 3, P], F32, name="expo")
             nc.scalar.activation(out=expo[:], in_=logit_sb[:], func=FUNC.Exp)
+            return expo, tanh_half
+
+        def normalise(expo, tanh_half):
             total = soft.tile([P, P], F32, name="total")
             nc.vector.tensor_add(out=total[:], in0=expo[:, 0, :], in1=expo[:, 1, :])
             nc.vector.tensor_add(out=total[:], in0=total[:], in1=expo[:, 2, :])
@@ -154,7 +165,6 @@ def tile_stackrnn_pb_kernel(
             nc.vector.reciprocal(out=inverse[:], in_=total[:])
             gates = gate_pool.tile([P, 3, P], F32, name="gates")
             nc.vector.tensor_mul(out=gates[:], in0=expo[:], in1=inverse[:].unsqueeze(1).to_broadcast(over_actions))
-
             top = soft.tile([P, P], F32, name="top")
             nc.vector.tensor_scalar(out=top[:], in0=tanh_half[:], scalar1=0.5, scalar2=0.5, op0=ALU.mult, op1=ALU.add)
             edges = gate_pool.tile([P, 2, P], F32, name="edges")
@@ -162,28 +172,35 @@ def tile_stackrnn_pb_kernel(
             nc.vector.tensor_scalar_mul(out=edges[:, 1, :], in0=gates[:, POP, :], scalar1=-1.0)
             return gates, edges
 
-        def multiply_group(t, j, x_sb, gates, terms):
-            first = j * ROWS
-            xT = psum.tile([P, ROWS, P], BF16, name="xT", tag="xT", bufs=2)
+        made = []
+        terms_of = []
+
+        def multiply(t, g):
+            x_sb = tiles_in[t][1]
+            gates = made[t][0]
+            first = g * ROWS
+            xT = psum.tile([P, ROWS, P], BF16, name="xT", tag="xT", bufs=3)
             for i in range(ROWS):
                 nc.tensor.transpose(xT[:, i, :], x_sb[:, first + i, :], ident_bf16[:])
             shape = [P, 3, ROWS, P]
-            product = terms[:, :, first : first + ROWS, :]
+            product = terms_of[t][:, :, first : first + ROWS, :]
             gate_view = gates[:].unsqueeze(2).to_broadcast(shape)
-            if (t * GROUPS + j) % 3 == 1:
+            if g < VECTOR_GROUPS:
+                nc.vector.tensor_tensor(out=product, in0=xT[:].unsqueeze(1).to_broadcast(shape), in1=gate_view, op=ALU.mult)
+            else:
                 xT_sb = stage.tile([P, ROWS, P], BF16, name="xT_sb")
                 nc.scalar.copy(out=xT_sb[:], in_=xT[:])
                 nc.gpsimd.tensor_tensor(out=product, in0=xT_sb[:].unsqueeze(1).to_broadcast(shape), in1=gate_view, op=ALU.mult)
-            else:
-                nc.vector.tensor_tensor(out=product, in0=xT[:].unsqueeze(1).to_broadcast(shape), in1=gate_view, op=ALU.mult)
 
-        def add_group(t, j, terms, edges):
+        def add_pair(t, j):
             rows = slice(t * P, (t + 1) * P)
-            new_sb = stage.tile([P, ROWS, S], F32, name="new_sb")
-            for part in range(ROWS // BANK_ROWS):
-                new_ps = psum.tile([P, BANK_ROWS, S], F32, name="new_ps", tag="new_ps", bufs=3)
-                for i in range(BANK_ROWS):
-                    d = j * ROWS + part * BANK_ROWS + i
+            terms = terms_of[t]
+            edges = made[t][1]
+            new_sb = stage.tile([P, PAIR, S], F32, name="new_sb")
+            for part in range(PAIR // ROWS):
+                new_ps = psum.tile([P, ROWS, S], F32, name="new_ps", tag="new_ps", bufs=2)
+                for i in range(ROWS):
+                    d = j * PAIR + part * ROWS + i
                     pushed = edges[:, 0, :] if d == 0 else terms[:, PUSH, d - 1, :]
                     popped = edges[:, 1, :] if d == DEPTH - 1 else terms[:, POP, d + 1, :]
                     summands = (pushed, terms[:, KEEP, d, :], popped)
@@ -196,20 +213,39 @@ def tile_stackrnn_pb_kernel(
                             start=(n == 0),
                             stop=(n == len(summands) - 1),
                         )
-                nc.scalar.copy(out=new_sb[:, part * BANK_ROWS : (part + 1) * BANK_ROWS, :], in_=new_ps[:])
-            nc.scalar.dma_start(out=out_1[rows, j * ROWS : (j + 1) * ROWS, :], in_=new_sb[:])
+                nc.scalar.copy(out=new_sb[:, part * ROWS : (part + 1) * ROWS, :], in_=new_ps[:])
+            nc.scalar.dma_start(out=out_1[rows, j * PAIR : (j + 1) * PAIR, :], in_=new_sb[:])
 
-        h_sb, x_sb = first_loads
-        gates, edges = gates_and_out(0, h_sb)
+        codes = quantise_h(0)
+        logits = matmuls(0, *codes)
+        parts = exponentials(logits)
+        made.append(normalise(*parts))
+        tiles_in.append(load_tile(1))
         for t in range(B_TILES):
-            if t + 1 < B_TILES:
-                next_h, next_x = load_tile(t + 1)
-                next_gates, next_edges = gates_and_out(t + 1, next_h)
-            terms = term_pool.tile([P, 3, DEPTH, P], F32, name="terms")
-            for j in range(GROUPS):
-                multiply_group(t, j, x_sb, gates, terms)
-                if j > 0:
-                    add_group(t, j - 1, terms, edges)
-            add_group(t, GROUPS - 1, terms, edges)
-            if t + 1 < B_TILES:
-                x_sb, gates, edges = next_x, next_gates, next_edges
+            ahead = t + 1 < B_TILES
+            if t + 2 < B_TILES:
+                tiles_in.append(load_tile(t + 2))
+            terms_of.append(term_pool.tile([P, 3, DEPTH, P], F32, name="terms"))
+            for g in range(VECTOR_GROUPS, GROUPS):
+                multiply(t, g)
+            multiply(t, 0)
+            if ahead:
+                codes = quantise_h(t + 1)
+            multiply(t, 1)
+            if t > 0:
+                add_pair(t - 1, 2)
+            if ahead:
+                logits = matmuls(t + 1, *codes)
+            multiply(t, 2)
+            if t > 0:
+                add_pair(t - 1, 3)
+            if ahead:
+                parts = exponentials(logits)
+            multiply(t, 3)
+            add_pair(t, 0)
+            multiply(t, 4)
+            if ahead:
+                made.append(normalise(*parts))
+            add_pair(t, 1)
+        add_pair(B_TILES - 1, 2)
+        add_pair(B_TILES - 1, 3)

@@ -198,6 +198,16 @@ def tile_stackrnn_pb_kernel(
             edges = made[t][1]
             new_sb = stage.tile([P, PAIR, S], F32, name="new_sb")
             for part in range(PAIR // ROWS):
+                idle_ps = psum.tile([P, N_OUT], F32, name="idle_ps", tag="hT")
+                nc.tensor.matmul_mx(
+                    out=idle_ps[:],
+                    lhsT=w_codes[:, 0, 0:P].bitcast(FP8X4),
+                    lhsT_scale=w_scales[:, 0, 0:P],
+                    rhs=w_codes[:, 0, N_GATES:].bitcast(FP8X4),
+                    rhs_scale=w_scales[:, 0, N_GATES:],
+                    start=True,
+                    stop=True,
+                )
                 new_ps = psum.tile([P, ROWS, S], F32, name="new_ps", tag="new_ps", bufs=2)
                 for i in range(ROWS):
                     d = j * PAIR + part * ROWS + i

@@ -25,7 +25,7 @@ B_TILES = BATCH // P
 PUSH, POP, KEEP = 0, 1, 2
 ROWS = 4
 GROUPS = DEPTH // ROWS
-VECTOR_GROUPS = 5
+VECTOR_GROUPS = 8
 PAIR = 2 * ROWS
 PAIRS = DEPTH // PAIR
 
@@ -198,16 +198,6 @@ def tile_stackrnn_pb_kernel(
             edges = made[t][1]
             new_sb = stage.tile([P, PAIR, S], F32, name="new_sb")
             for part in range(PAIR // ROWS):
-                idle_ps = psum.tile([P, N_OUT], F32, name="idle_ps", tag="hT")
-                nc.tensor.matmul_mx(
-                    out=idle_ps[:],
-                    lhsT=w_codes[:, 0, 0:P].bitcast(FP8X4),
-                    lhsT_scale=w_scales[:, 0, 0:P],
-                    rhs=w_codes[:, 0, N_GATES:].bitcast(FP8X4),
-                    rhs_scale=w_scales[:, 0, N_GATES:],
-                    start=True,
-                    stop=True,
-                )
                 new_ps = psum.tile([P, ROWS, S], F32, name="new_ps", tag="new_ps", bufs=2)
                 for i in range(ROWS):
                     d = j * PAIR + part * ROWS + i
@@ -236,26 +226,18 @@ def tile_stackrnn_pb_kernel(
             if t + 2 < B_TILES:
                 tiles_in.append(load_tile(t + 2))
             terms_of.append(term_pool.tile([P, 3, DEPTH, P], F32, name="terms"))
-            for g in range(VECTOR_GROUPS, GROUPS):
+            for g in range(GROUPS):
                 multiply(t, g)
-            multiply(t, 0)
-            if ahead:
-                codes = quantise_h(t + 1)
-            multiply(t, 1)
-            if t > 0:
-                add_pair(t - 1, 2)
-            if ahead:
-                logits = matmuls(t + 1, *codes)
-            multiply(t, 2)
-            if t > 0:
-                add_pair(t - 1, 3)
-            if ahead:
-                parts = exponentials(logits)
-            multiply(t, 3)
-            add_pair(t, 0)
-            multiply(t, 4)
-            if ahead:
-                made.append(normalise(*parts))
-            add_pair(t, 1)
-        add_pair(B_TILES - 1, 2)
-        add_pair(B_TILES - 1, 3)
+                if g == 0 and t > 0:
+                    add_pair(t - 1, PAIRS - 1)
+                if g >= 2 and g % 2 == 0:
+                    add_pair(t, g // 2 - 1)
+                if ahead and g == 0:
+                    codes = quantise_h(t + 1)
+                if ahead and g == 1:
+                    logits = matmuls(t + 1, *codes)
+                if ahead and g == 3:
+                    parts = exponentials(logits)
+                if ahead and g == 5:
+                    made.append(normalise(*parts))
+        add_pair(B_TILES - 1, PAIRS - 1)

@@ -25,9 +25,11 @@ B_TILES = BATCH // P
 PUSH, POP, KEEP = 0, 1, 2
 ROWS = 4
 GROUPS = DEPTH // ROWS
-VECTOR_GROUPS = 8
-PAIR = 2 * ROWS
-PAIRS = DEPTH // PAIR
+BANK_ROWS = 2 * ROWS
+BANKS = DEPTH // BANK_ROWS
+POOL_BANK = BANKS - 1
+VECTOR_GROUPS = GROUPS - 2
+AHEAD = 5
 
 FLOPS = 2 * BATCH * K * (N_GATES + N_OUT)
 
@@ -38,7 +40,7 @@ def tile_stackrnn_pb_kernel(
     nc = tc.nc
     with ExitStack() as ctx:
         const = ctx.enter_context(tc.tile_pool(name="const", bufs=1))
-        loads = ctx.enter_context(tc.tile_pool(name="loads", bufs=4))
+        loads = ctx.enter_context(tc.tile_pool(name="loads", bufs=AHEAD + 1))
         quant = ctx.enter_context(tc.tile_pool(name="quant", bufs=2))
         soft = ctx.enter_context(tc.tile_pool(name="soft", bufs=2))
         gate_pool = ctx.enter_context(tc.tile_pool(name="gates", bufs=3))
@@ -46,18 +48,24 @@ def tile_stackrnn_pb_kernel(
         stage = ctx.enter_context(tc.tile_pool(name="stage", bufs=4))
         psum = ctx.enter_context(tc.psum_pool(name="psum", bufs=1))
 
+        h_of, x_of = {}, {}
+
+        def load_h(t, queue):
+            h_of[t] = loads.tile([P, K], BF16, name="h_sb")
+            queue.dma_start(out=h_of[t][:], in_=h[t * P : (t + 1) * P, :])
+
+        def load_x(t):
+            x_of[t] = loads.tile([P, DEPTH, S], BF16, name="x_sb")
+            nc.sync.dma_start(out=x_of[t][:], in_=stack[t * P : (t + 1) * P, :, :])
+
+        load_h(0, nc.scalar)
+
         ident_f32 = const.tile([P, P], F32, name="ident_f32")
         make_identity(nc, ident_f32[:])
         ident_bf16 = const.tile([P, P], BF16, name="ident_bf16")
         make_identity(nc, ident_bf16[:])
-
-        def load_tile(t):
-            rows = slice(t * P, (t + 1) * P)
-            h_sb = loads.tile([P, K], BF16, name="h_sb")
-            nc.sync.dma_start(out=h_sb[:], in_=h[rows, :])
-            x_sb = loads.tile([P, DEPTH, S], BF16, name="x_sb")
-            nc.sync.dma_start(out=x_sb[:], in_=stack[rows, :, :])
-            return h_sb, x_sb
+        warm = const.tile([P, 1], F32, name="warm")
+        nc.scalar.activation(out=warm[:], in_=ident_f32[:, 0:1], func=FUNC.Exp)
 
         w_codes = const.tile([P, PASSES, N_GATES + N_OUT], U32, name="w_codes", align_bytes=64)
         w_scales = const.tile([P, PASSES, N_GATES + N_OUT], U8, name="w_scales", align_bytes=64)
@@ -65,40 +73,57 @@ def tile_stackrnn_pb_kernel(
         bias_rows = const.tile([P, P], BF16, name="bias_rows")
         nc.vector.memset(bias_rows[:].bitcast(I32), 0)
 
-        tiles_in = [load_tile(0)]
         weights = ((Wa_words, Wa_scales, 0, 3 * S), (Ws_words, Ws_scales, 3 * S, S), (Wo_words, Wo_scales, N_GATES, N_OUT))
-        for words, scales, first, width in weights:
-            nc.sync.dma_start(
-                out=w_codes[:, :, first : first + width].bitcast(I32),
-                in_=words.rearrange("g p n t -> p g (n t)").bitcast(I32),
-            )
         for words, scales, first, width in weights:
             for quad in range(4):
                 nc.sync.dma_start(
                     out=w_scales[32 * quad : 32 * quad + 4, :, first : first + width].bitcast(I32),
                     in_=scales[:, 4 * quad : 4 * quad + 4, :].rearrange("g r n -> r g n").bitcast(I32),
                 )
-
-        nc.sync.dma_start(out=bias_rows[0:3, :], in_=ba.rearrange("(a s) -> a s", a=3))
-        nc.sync.dma_start(out=bias_rows[3:4, :], in_=bs.rearrange("(a s) -> a s", a=1))
-        bias_ps = psum.tile([P, P], BF16, name="bias_ps", tag="hT")
-        nc.tensor.transpose(bias_ps[:], bias_rows[:], ident_bf16[:])
-        bias_col = const.tile([P, 4], F32, name="bias_col")
-        nc.vector.tensor_copy(out=bias_col[:], in_=bias_ps[:, 0:4])
-        half_bs = const.tile([P, 1], F32, name="half_bs")
-        nc.vector.tensor_scalar_mul(out=half_bs[:], in0=bias_col[:, 3:4], scalar1=0.5)
+        nc.scalar.dma_start(out=bias_rows[0:3, :], in_=ba.rearrange("(a s) -> a s", a=3))
+        nc.scalar.dma_start(out=bias_rows[3:4, :], in_=bs.rearrange("(a s) -> a s", a=1))
+        for words, scales, first, width in weights:
+            nc.sync.dma_start(
+                out=w_codes[:, :, first : first + width].bitcast(I32),
+                in_=words.rearrange("g p n t -> p g (n t)").bitcast(I32),
+            )
+        load_x(0)
+        load_h(1, nc.sync)
         bo_all = const.tile([P, N_OUT], BF16, name="bo_all")
         nc.sync.dma_start(out=bo_all[:], in_=bo.partition_broadcast(P))
+        load_x(1)
+        for t in range(2, AHEAD):
+            load_h(t, nc.sync)
+            load_x(t)
+        bias_col = const.tile([P, 4], F32, name="bias_col")
+        half_bs = const.tile([P, 1], F32, name="half_bs")
 
-        def quantise_h(t):
-            h_sb = tiles_in[t][0]
-            h_words = h_sb[:].bitcast(F32)
-            hT = psum.tile([P, PASSES, 2, P], F32, name="hT", tag="hT")
+        def turn_biases():
+            bias_ps = psum.tile([P, P], BF16, name="bias_ps", tag="bank_b")
+            nc.tensor.transpose(bias_ps[:], bias_rows[:], ident_bf16[:])
+            nc.vector.tensor_copy(out=bias_col[:], in_=bias_ps[:, 0:4])
+            nc.vector.tensor_scalar_mul(out=half_bs[:], in0=bias_col[:, 3:4], scalar1=0.5)
+
+        over_actions = [P, 3, P]
+        part = {}
+        sums_of = {}
+
+        def turn_h(t):
+            h_words = h_of[t][:].bitcast(F32)
+            hT = psum.tile([P, PASSES, 2, P], F32, name="hT", tag="bank_a")
             for g in range(PASSES):
                 for u in range(2):
                     nc.tensor.transpose(hT[:, g, u, :], h_words[:, 256 * g + u : 256 * (g + 1) : 2], ident_f32[:])
+            part[t] = hT
+
+        def group_h(t):
+            hT = part[t]
             grouped = quant.tile([P, PASSES, P, 4], BF16, name="grouped", align_bytes=64)
             nc.scalar.copy(out=grouped[:].bitcast(F32), in_=hT[:].rearrange("p g u b -> p g b u"))
+            part[t] = grouped
+
+        def quantise_h(t):
+            grouped = part[t]
             h_codes = quant.tile([P, PASSES, P], U32, name="h_codes", align_bytes=64)
             h_scales = quant.tile([P, PASSES, P], U8, name="h_scales", align_bytes=64)
             nc.vector.quantize_mx(
@@ -106,11 +131,11 @@ def tile_stackrnn_pb_kernel(
                 scales=h_scales[:].rearrange("p g b -> p (g b)"),
                 in_=grouped[:].rearrange("p g b t -> p (g b t)"),
             )
-            return h_codes, h_scales
+            part[t] = (h_codes, h_scales)
 
-        def matmuls(t, h_codes, h_scales):
-            rows = slice(t * P, (t + 1) * P)
-            logits = psum.tile([P, 4, P], F32, name="logits", tag="logits")
+        def matmuls(t):
+            h_codes, h_scales = part[t]
+            logits = psum.tile([P, 4, P], F32, name="logits", tag="bank_b")
             for j in range(4):
                 cols = slice(j * S, (j + 1) * S)
                 for g in range(PASSES):
@@ -123,7 +148,7 @@ def tile_stackrnn_pb_kernel(
                         start=(g == 0),
                         stop=(g == PASSES - 1),
                     )
-            out_ps = psum.tile([P, N_OUT], F32, name="out_ps", tag="out_ps")
+            out_ps = psum.tile([P, N_OUT], F32, name="out_ps", tag="bank_a")
             for g in range(PASSES):
                 nc.tensor.matmul_mx(
                     out=out_ps[:],
@@ -134,14 +159,11 @@ def tile_stackrnn_pb_kernel(
                     start=(g == 0),
                     stop=(g == PASSES - 1),
                 )
-            out_sb = stage.tile([P, N_OUT], F32, name="out_sb")
-            nc.vector.tensor_add(out=out_sb[:], in0=out_ps[:], in1=bo_all[:])
-            nc.sync.dma_start(out=out_0[rows, :], in_=out_sb[:])
-            return logits
+            part[t] = logits
+            sums_of[t] = out_ps
 
-        over_actions = [P, 3, P]
-
-        def exponentials(logits):
+        def biased(t):
+            logits = part[t]
             logit_sb = soft.tile([P, 3, P], F32, name="logit_sb")
             for a in range(3):
                 nc.scalar.activation(
@@ -149,95 +171,211 @@ def tile_stackrnn_pb_kernel(
                 )
             tanh_half = soft.tile([P, P], F32, name="tanh_half")
             nc.scalar.activation(out=tanh_half[:], in_=logits[:, 3, :], func=FUNC.Tanh, bias=half_bs[:], scale=0.5)
-            peak = soft.tile([P, P], F32, name="peak")
-            nc.vector.tensor_max(out=peak[:], in0=logit_sb[:, 0, :], in1=logit_sb[:, 1, :])
-            nc.vector.tensor_max(out=peak[:], in0=peak[:], in1=logit_sb[:, 2, :])
-            nc.vector.tensor_sub(out=logit_sb[:], in0=logit_sb[:], in1=peak[:].unsqueeze(1).to_broadcast(over_actions))
-            expo = soft.tile([P, 3, P], F32, name="expo")
-            nc.scalar.activation(out=expo[:], in_=logit_sb[:], func=FUNC.Exp)
-            return expo, tanh_half
+            part[t] = (logits, logit_sb, tanh_half)
 
-        def normalise(expo, tanh_half):
+        def store_out(t):
+            out_ps = sums_of[t]
+            out_sb = stage.tile([P, N_OUT], F32, name="out_sb", bufs=2)
+            nc.vector.tensor_add(out=out_sb[:], in0=out_ps[:], in1=bo_all[:])
+            nc.sync.dma_start(out=out_0[t * P : (t + 1) * P, :], in_=out_sb[:])
+
+        def peak_of(t):
+            logits, logit_sb, tanh_half = part[t]
+            peak01 = soft.tile([P, P], F32, name="peak01")
+            nc.vector.scalar_tensor_tensor(
+                out=peak01[:], in0=logits[:, 0, :], scalar=bias_col[:, 0:1], in1=logit_sb[:, 1, :], op0=ALU.add, op1=ALU.max
+            )
+            peak = soft.tile([P, P], F32, name="peak")
+            nc.vector.scalar_tensor_tensor(
+                out=peak[:], in0=logits[:, 2, :], scalar=bias_col[:, 2:3], in1=peak01[:], op0=ALU.add, op1=ALU.max
+            )
+            part[t] = (logit_sb, tanh_half, peak)
+
+        def shift(t, engine):
+            logit_sb, tanh_half, peak = part[t]
+            shifted = soft.tile([P, 3, P], F32, name="shifted")
+            engine.tensor_tensor(
+                out=shifted[:], in0=logit_sb[:], in1=peak[:].unsqueeze(1).to_broadcast(over_actions), op=ALU.subtract
+            )
+            part[t] = (tanh_half, shifted)
+
+        def exponentials(t):
+            tanh_half, shifted = part[t]
+            expo = soft.tile([P, 3, P], F32, name="expo")
+            nc.scalar.activation(out=expo[:], in_=shifted[:], func=FUNC.Exp)
+            top = soft.tile([P, P], F32, name="top")
+            nc.scalar.activation(out=top[:], in_=tanh_half[:], func=FUNC.Copy, bias=0.5, scale=0.5)
+            part[t] = (top, expo)
+
+        def total_of(t, engine):
+            top, expo = part[t]
+            total01 = soft.tile([P, P], F32, name="total01")
+            engine.tensor_tensor(out=total01[:], in0=expo[:, 0, :], in1=expo[:, 1, :], op=ALU.add)
             total = soft.tile([P, P], F32, name="total")
-            nc.vector.tensor_add(out=total[:], in0=expo[:, 0, :], in1=expo[:, 1, :])
-            nc.vector.tensor_add(out=total[:], in0=total[:], in1=expo[:, 2, :])
+            engine.tensor_tensor(out=total[:], in0=total01[:], in1=expo[:, 2, :], op=ALU.add)
+            part[t] = (top, expo, total)
+
+        def invert(t):
+            top, expo, total = part[t]
             inverse = soft.tile([P, P], F32, name="inverse")
             nc.vector.reciprocal(out=inverse[:], in_=total[:])
+            part[t] = (top, expo, inverse)
+
+        made = {}
+
+        def normalise(t, engine):
+            top, expo, inverse = part[t]
             gates = gate_pool.tile([P, 3, P], F32, name="gates")
-            nc.vector.tensor_mul(out=gates[:], in0=expo[:], in1=inverse[:].unsqueeze(1).to_broadcast(over_actions))
-            top = soft.tile([P, P], F32, name="top")
-            nc.vector.tensor_scalar(out=top[:], in0=tanh_half[:], scalar1=0.5, scalar2=0.5, op0=ALU.mult, op1=ALU.add)
+            engine.tensor_tensor(
+                out=gates[:], in0=expo[:], in1=inverse[:].unsqueeze(1).to_broadcast(over_actions), op=ALU.mult
+            )
+            part[t] = (top, gates)
+
+        def edge_rows(t, engine):
+            top, gates = part[t]
             edges = gate_pool.tile([P, 2, P], F32, name="edges")
-            nc.vector.tensor_mul(out=edges[:, 0, :], in0=gates[:, PUSH, :], in1=top[:])
-            nc.vector.tensor_scalar_mul(out=edges[:, 1, :], in0=gates[:, POP, :], scalar1=-1.0)
-            return gates, edges
+            engine.tensor_tensor(out=edges[:, 0, :], in0=gates[:, PUSH, :], in1=top[:], op=ALU.mult)
+            nc.scalar.mul(out=edges[:, 1, :], in_=gates[:, POP, :], mul=-1.0)
+            made[t] = (gates, edges)
 
-        made = []
-        terms_of = []
+        turned = {}
+        terms_of = {}
+        staged = {}
 
-        def multiply(t, g):
-            x_sb = tiles_in[t][1]
-            gates = made[t][0]
-            first = g * ROWS
-            xT = psum.tile([P, ROWS, P], BF16, name="xT", tag="xT", bufs=3)
-            for i in range(ROWS):
-                nc.tensor.transpose(xT[:, i, :], x_sb[:, first + i, :], ident_bf16[:])
-            shape = [P, 3, ROWS, P]
-            product = terms_of[t][:, :, first : first + ROWS, :]
-            gate_view = gates[:].unsqueeze(2).to_broadcast(shape)
-            if g < VECTOR_GROUPS:
-                nc.vector.tensor_tensor(out=product, in0=xT[:].unsqueeze(1).to_broadcast(shape), in1=gate_view, op=ALU.mult)
-            else:
-                xT_sb = stage.tile([P, ROWS, P], BF16, name="xT_sb")
+        def forward(t, bank):
+            xT = psum.tile([P, BANK_ROWS, P], BF16, name="xT", tag="xT", bufs=3)
+            for i in range(BANK_ROWS):
+                nc.tensor.transpose(xT[:, i, :], x_of[t][:, bank * BANK_ROWS + i, :], ident_bf16[:])
+            turned[t, bank] = xT
+            if bank == POOL_BANK:
+                xT_sb = stage.tile([P, BANK_ROWS, P], BF16, name="xT_sb", bufs=2)
                 nc.scalar.copy(out=xT_sb[:], in_=xT[:])
-                nc.gpsimd.tensor_tensor(out=product, in0=xT_sb[:].unsqueeze(1).to_broadcast(shape), in1=gate_view, op=ALU.mult)
+                turned[t, bank] = xT_sb
 
-        def add_pair(t, j):
-            rows = slice(t * P, (t + 1) * P)
+        def multiply_vector(t, g):
+            first = (g % 2) * ROWS
+            shape = [P, 3, ROWS, P]
+            nc.vector.tensor_tensor(
+                out=terms_of[t][:, :, g * ROWS : (g + 1) * ROWS, :],
+                in0=turned[t, g // 2][:, first : first + ROWS, :].unsqueeze(1).to_broadcast(shape),
+                in1=made[t][0][:].unsqueeze(2).to_broadcast(shape),
+                op=ALU.mult,
+            )
+
+        def multiply_pool(t, g, a):
+            first = (g % 2) * ROWS
+            nc.gpsimd.tensor_tensor(
+                out=terms_of[t][:, a, g * ROWS : (g + 1) * ROWS, :],
+                in0=turned[t, g // 2][:, first : first + ROWS, :],
+                in1=made[t][0][:, a, :].unsqueeze(1).to_broadcast([P, ROWS, P]),
+                op=ALU.mult,
+            )
+
+        pool_units = [(g, a) for g in range(VECTOR_GROUPS, GROUPS) for a in (POP, KEEP, PUSH)]
+
+        def back(t, g):
             terms = terms_of[t]
             edges = made[t][1]
-            new_sb = stage.tile([P, PAIR, S], F32, name="new_sb")
-            for part in range(PAIR // ROWS):
-                new_ps = psum.tile([P, ROWS, S], F32, name="new_ps", tag="new_ps", bufs=2)
-                for i in range(ROWS):
-                    d = j * PAIR + part * ROWS + i
-                    pushed = edges[:, 0, :] if d == 0 else terms[:, PUSH, d - 1, :]
-                    popped = edges[:, 1, :] if d == DEPTH - 1 else terms[:, POP, d + 1, :]
-                    summands = (pushed, terms[:, KEEP, d, :], popped)
-                    for n, term in enumerate(summands):
-                        nc.tensor.matmul(
-                            out=new_ps[:, i, :],
-                            lhsT=term,
-                            rhs=ident_f32[:],
-                            is_transpose=True,
-                            start=(n == 0),
-                            stop=(n == len(summands) - 1),
-                        )
-                nc.scalar.copy(out=new_sb[:, part * ROWS : (part + 1) * ROWS, :], in_=new_ps[:])
-            nc.scalar.dma_start(out=out_1[rows, j * PAIR : (j + 1) * PAIR, :], in_=new_sb[:])
+            if g % 2 == 0:
+                staged[t] = stage.tile([P, 2 * ROWS, S], F32, name="new_sb")
+            new_sb = staged[t]
+            new_ps = psum.tile([P, ROWS, S], F32, name="new_ps", tag="new_ps", bufs=3)
+            for i in range(ROWS):
+                d = g * ROWS + i
+                pushed = edges[:, 0, :] if d == 0 else terms[:, PUSH, d - 1, :]
+                popped = edges[:, 1, :] if d == DEPTH - 1 else terms[:, POP, d + 1, :]
+                summands = (pushed, terms[:, KEEP, d, :], popped)
+                for n, term in enumerate(summands):
+                    nc.tensor.matmul(
+                        out=new_ps[:, i, :],
+                        lhsT=term,
+                        rhs=ident_f32[:],
+                        is_transpose=True,
+                        start=(n == 0),
+                        stop=(n == len(summands) - 1),
+                    )
+            nc.scalar.copy(out=new_sb[:, (g % 2) * ROWS : (g % 2 + 1) * ROWS, :], in_=new_ps[:])
+            if g % 2 == 1:
+                nc.sync.dma_start(out=out_1[t * P : (t + 1) * P, (g - 1) * ROWS : (g + 1) * ROWS, :], in_=new_sb[:])
 
-        codes = quantise_h(0)
-        logits = matmuls(0, *codes)
-        parts = exponentials(logits)
-        made.append(normalise(*parts))
-        tiles_in.append(load_tile(1))
+        ctx.enter_context(tc.manual_schedule())
+        turn_h(0)
+        group_h(0)
+        quantise_h(0)
+        turn_biases()
+        matmuls(0)
+        biased(0)
+        peak_of(0)
+        shift(0, nc.vector)
+        exponentials(0)
+        total_of(0, nc.vector)
+        invert(0)
+        normalise(0, nc.vector)
+        edge_rows(0, nc.vector)
+        forward(0, POOL_BANK)
+        forward(0, 0)
+        forward(0, 1)
+        store_out(0)
+        turn_h(1)
+        group_h(1)
+        quantise_h(1)
+        matmuls(1)
+        biased(1)
+        store_out(1)
+
         for t in range(B_TILES):
-            ahead = t + 1 < B_TILES
-            if t + 2 < B_TILES:
-                tiles_in.append(load_tile(t + 2))
-            terms_of.append(term_pool.tile([P, 3, DEPTH, P], F32, name="terms"))
-            for g in range(GROUPS):
-                multiply(t, g)
-                if g == 0 and t > 0:
-                    add_pair(t - 1, PAIRS - 1)
-                if g >= 2 and g % 2 == 0:
-                    add_pair(t, g // 2 - 1)
-                if ahead and g == 0:
-                    codes = quantise_h(t + 1)
-                if ahead and g == 1:
-                    logits = matmuls(t + 1, *codes)
-                if ahead and g == 3:
-                    parts = exponentials(logits)
-                if ahead and g == 5:
-                    made.append(normalise(*parts))
-        add_pair(B_TILES - 1, PAIRS - 1)
+            soon = t + 1 if t + 1 < B_TILES else None
+            later = t + 2 if t + 2 < B_TILES else None
+            if t + AHEAD < B_TILES:
+                load_h(t + AHEAD, nc.sync)
+                load_x(t + AHEAD)
+            terms_of[t] = term_pool.tile([P, 3, DEPTH, P], F32, name="terms")
+            for j in range(VECTOR_GROUPS):
+                if j == 0:
+                    forward(t, 2)
+                if soon is not None and j in (2, 3, 4):
+                    forward(soon, (POOL_BANK, 0, 1)[j - 2])
+                multiply_vector(t, j)
+                multiply_pool(t, *pool_units[j])
+                if j == 0:
+                    if soon is not None:
+                        peak_of(soon)
+                    if t > 0:
+                        back(t - 1, 4)
+                        back(t - 1, 5)
+                if j == 1:
+                    if soon is not None:
+                        shift(soon, nc.gpsimd)
+                    if later is not None:
+                        turn_h(later)
+                    if t > 0:
+                        back(t - 1, 6)
+                    if soon is not None:
+                        exponentials(soon)
+                    if t > 0:
+                        back(t - 1, 7)
+                    if later is not None:
+                        group_h(later)
+                if j == 2:
+                    if soon is not None:
+                        total_of(soon, nc.gpsimd)
+                if j == 3:
+                    if soon is not None:
+                        invert(soon)
+                    if later is not None:
+                        quantise_h(later)
+                if j == 4:
+                    if soon is not None:
+                        normalise(soon, nc.gpsimd)
+                    if later is not None:
+                        matmuls(later)
+                if j >= 2:
+                    back(t, j - 2)
+                if j == 5:
+                    if soon is not None:
+                        edge_rows(soon, nc.gpsimd)
+                    if later is not None:
+                        biased(later)
+                        store_out(later)
+        for g in range(VECTOR_GROUPS - 2, GROUPS):
+            back(B_TILES - 1, g)

@@ -29,6 +29,7 @@ BANK_ROWS = 2 * ROWS
 BANKS = DEPTH // BANK_ROWS
 POOL_BANK = BANKS - 1
 VECTOR_GROUPS = GROUPS - 2
+COUNTED_GROUPS = (0, 1, 2, 3, 4, 6)
 AHEAD = 5
 
 FLOPS = 2 * BATCH * K * (N_GATES + N_OUT)
@@ -59,6 +60,7 @@ def tile_stackrnn_pb_kernel(
             nc.sync.dma_start(out=x_of[t][:], in_=stack[t * P : (t + 1) * P, :, :])
 
         load_h(0, nc.scalar)
+        load_h(1, nc.scalar)
 
         ident_f32 = const.tile([P, P], F32, name="ident_f32")
         make_identity(nc, ident_f32[:])
@@ -73,22 +75,24 @@ def tile_stackrnn_pb_kernel(
         bias_rows = const.tile([P, P], BF16, name="bias_rows")
         nc.vector.memset(bias_rows[:].bitcast(I32), 0)
 
-        weights = ((Wa_words, Wa_scales, 0, 3 * S), (Ws_words, Ws_scales, 3 * S, S), (Wo_words, Wo_scales, N_GATES, N_OUT))
-        for words, scales, first, width in weights:
-            for quad in range(4):
+        def load_weights(weights):
+            for words, scales, first, width in weights:
+                for quad in range(4):
+                    nc.sync.dma_start(
+                        out=w_scales[32 * quad : 32 * quad + 4, :, first : first + width].bitcast(I32),
+                        in_=scales[:, 4 * quad : 4 * quad + 4, :].rearrange("g r n -> r g n").bitcast(I32),
+                    )
+            for words, scales, first, width in weights:
                 nc.sync.dma_start(
-                    out=w_scales[32 * quad : 32 * quad + 4, :, first : first + width].bitcast(I32),
-                    in_=scales[:, 4 * quad : 4 * quad + 4, :].rearrange("g r n -> r g n").bitcast(I32),
+                    out=w_codes[:, :, first : first + width].bitcast(I32),
+                    in_=words.rearrange("g p n t -> p g (n t)").bitcast(I32),
                 )
+
+        load_weights(((Wa_words, Wa_scales, 0, 3 * S), (Ws_words, Ws_scales, 3 * S, S)))
         nc.scalar.dma_start(out=bias_rows[0:3, :], in_=ba.rearrange("(a s) -> a s", a=3))
         nc.scalar.dma_start(out=bias_rows[3:4, :], in_=bs.rearrange("(a s) -> a s", a=1))
-        for words, scales, first, width in weights:
-            nc.sync.dma_start(
-                out=w_codes[:, :, first : first + width].bitcast(I32),
-                in_=words.rearrange("g p n t -> p g (n t)").bitcast(I32),
-            )
         load_x(0)
-        load_h(1, nc.sync)
+        load_weights(((Wo_words, Wo_scales, N_GATES, N_OUT),))
         bo_all = const.tile([P, N_OUT], BF16, name="bo_all")
         nc.sync.dma_start(out=bo_all[:], in_=bo.partition_broadcast(P))
         load_x(1)
@@ -106,6 +110,7 @@ def tile_stackrnn_pb_kernel(
 
         over_actions = [P, 3, P]
         part = {}
+        codes_of = {}
         sums_of = {}
 
         def turn_h(t):
@@ -124,17 +129,17 @@ def tile_stackrnn_pb_kernel(
 
         def quantise_h(t):
             grouped = part[t]
-            h_codes = quant.tile([P, PASSES, P], U32, name="h_codes", align_bytes=64)
-            h_scales = quant.tile([P, PASSES, P], U8, name="h_scales", align_bytes=64)
+            h_codes = quant.tile([P, PASSES, P], U32, name="h_codes", align_bytes=64, bufs=3)
+            h_scales = quant.tile([P, PASSES, P], U8, name="h_scales", align_bytes=64, bufs=3)
             nc.vector.quantize_mx(
                 out=h_codes[:].rearrange("p g b -> p (g b)").bitcast(FP8X4),
                 scales=h_scales[:].rearrange("p g b -> p (g b)"),
                 in_=grouped[:].rearrange("p g b t -> p (g b t)"),
             )
-            part[t] = (h_codes, h_scales)
+            codes_of[t] = (h_codes, h_scales)
 
-        def matmuls(t):
-            h_codes, h_scales = part[t]
+        def gate_matmuls(t):
+            h_codes, h_scales = codes_of[t]
             logits = psum.tile([P, 4, P], F32, name="logits", tag="bank_b")
             for j in range(4):
                 cols = slice(j * S, (j + 1) * S)
@@ -148,6 +153,10 @@ def tile_stackrnn_pb_kernel(
                         start=(g == 0),
                         stop=(g == PASSES - 1),
                     )
+            part[t] = logits
+
+        def out_matmuls(t):
+            h_codes, h_scales = codes_of[t]
             out_ps = psum.tile([P, N_OUT], F32, name="out_ps", tag="bank_a")
             for g in range(PASSES):
                 nc.tensor.matmul_mx(
@@ -159,7 +168,6 @@ def tile_stackrnn_pb_kernel(
                     start=(g == 0),
                     stop=(g == PASSES - 1),
                 )
-            part[t] = logits
             sums_of[t] = out_ps
 
         def biased(t):
@@ -290,7 +298,7 @@ def tile_stackrnn_pb_kernel(
                         out=new_ps[:, i, :],
                         lhsT=term,
                         rhs=ident_f32[:],
-                        is_transpose=True,
+                        is_transpose=not (g in COUNTED_GROUPS and i == 0 and n == 0),
                         start=(n == 0),
                         stop=(n == len(summands) - 1),
                     )
@@ -303,25 +311,23 @@ def tile_stackrnn_pb_kernel(
         group_h(0)
         quantise_h(0)
         turn_biases()
-        matmuls(0)
+        gate_matmuls(0)
+        turn_h(1)
         biased(0)
+        group_h(1)
+        forward(0, POOL_BANK)
         peak_of(0)
         shift(0, nc.vector)
+        quantise_h(1)
         exponentials(0)
+        forward(0, 0)
+        forward(0, 1)
         total_of(0, nc.vector)
         invert(0)
         normalise(0, nc.vector)
         edge_rows(0, nc.vector)
-        forward(0, POOL_BANK)
-        forward(0, 0)
-        forward(0, 1)
-        store_out(0)
-        turn_h(1)
-        group_h(1)
-        quantise_h(1)
-        matmuls(1)
+        gate_matmuls(1)
         biased(1)
-        store_out(1)
 
         for t in range(B_TILES):
             soon = t + 1 if t + 1 < B_TILES else None
@@ -368,7 +374,8 @@ def tile_stackrnn_pb_kernel(
                     if soon is not None:
                         normalise(soon, nc.gpsimd)
                     if later is not None:
-                        matmuls(later)
+                        gate_matmuls(later)
+                    out_matmuls(t)
                 if j >= 2:
                     back(t, j - 2)
                 if j == 5:
@@ -376,6 +383,6 @@ def tile_stackrnn_pb_kernel(
                         edge_rows(soon, nc.gpsimd)
                     if later is not None:
                         biased(later)
-                        store_out(later)
+                    store_out(t)
         for g in range(VECTOR_GROUPS - 2, GROUPS):
             back(B_TILES - 1, g)

@@ -366,13 +366,12 @@ def tile_stackrnn_pb_kernel(
                     if soon is not None:
                         total_of(soon, nc.gpsimd)
                 if j == 3:
-                    if soon is not None:
-                        invert(soon)
                     if later is not None:
                         quantise_h(later)
-                if j == 4:
                     if soon is not None:
+                        invert(soon)
                         normalise(soon, nc.gpsimd)
+                if j == 4:
                     if later is not None:
                         gate_matmuls(later)
                     out_matmuls(t)

@@ -29,7 +29,7 @@ BANK_ROWS = 2 * ROWS
 BANKS = DEPTH // BANK_ROWS
 POOL_BANK = BANKS - 1
 VECTOR_GROUPS = GROUPS - 2
-COUNTED_GROUPS = (0, 1, 2, 3, 4, 6)
+COUNTED_GROUPS = (0, 4, 6)
 AHEAD = 5
 
 FLOPS = 2 * BATCH * K * (N_GATES + N_OUT)

@@ -29,8 +29,8 @@ BANK_ROWS = 2 * ROWS
 BANKS = DEPTH // BANK_ROWS
 POOL_BANK = BANKS - 1
 VECTOR_GROUPS = GROUPS - 2
-COUNTED_GROUPS = (0, 4, 6)
-AHEAD = 5
+COUNTED_GROUPS = (0, 1, 3, 4, 6)
+AHEAD = 4
 
 FLOPS = 2 * BATCH * K * (N_GATES + N_OUT)
 
@@ -52,7 +52,7 @@ def tile_stackrnn_pb_kernel(
         h_of, x_of = {}, {}
 
         def load_h(t, queue):
-            h_of[t] = loads.tile([P, K], BF16, name="h_sb")
+            h_of[t] = loads.tile([P, K], BF16, name="h_sb", bufs=B_TILES // 2)
             queue.dma_start(out=h_of[t][:], in_=h[t * P : (t + 1) * P, :])
 
         def load_x(t):
@@ -91,19 +91,21 @@ def tile_stackrnn_pb_kernel(
         load_weights(((Wa_words, Wa_scales, 0, 3 * S), (Ws_words, Ws_scales, 3 * S, S)))
         nc.scalar.dma_start(out=bias_rows[0:3, :], in_=ba.rearrange("(a s) -> a s", a=3))
         nc.scalar.dma_start(out=bias_rows[3:4, :], in_=bs.rearrange("(a s) -> a s", a=1))
+        load_h(2, nc.sync)
+        load_h(3, nc.sync)
         load_x(0)
         load_weights(((Wo_words, Wo_scales, N_GATES, N_OUT),))
         bo_all = const.tile([P, N_OUT], BF16, name="bo_all")
         nc.sync.dma_start(out=bo_all[:], in_=bo.partition_broadcast(P))
-        load_x(1)
-        for t in range(2, AHEAD):
+        for t in range(4, B_TILES):
             load_h(t, nc.sync)
+        for t in range(1, AHEAD):
             load_x(t)
         bias_col = const.tile([P, 4], F32, name="bias_col")
         half_bs = const.tile([P, 1], F32, name="half_bs")
 
         def turn_biases():
-            bias_ps = psum.tile([P, P], BF16, name="bias_ps", tag="bank_b")
+            bias_ps = psum.tile([P, P], BF16, name="bias_ps", tag="bank_a")
             nc.tensor.transpose(bias_ps[:], bias_rows[:], ident_bf16[:])
             nc.vector.tensor_copy(out=bias_col[:], in_=bias_ps[:, 0:4])
             nc.vector.tensor_scalar_mul(out=half_bs[:], in0=bias_col[:, 3:4], scalar1=0.5)
@@ -113,9 +115,9 @@ def tile_stackrnn_pb_kernel(
         codes_of = {}
         sums_of = {}
 
-        def turn_h(t):
+        def turn_h(t, bank):
             h_words = h_of[t][:].bitcast(F32)
-            hT = psum.tile([P, PASSES, 2, P], F32, name="hT", tag="bank_a")
+            hT = psum.tile([P, PASSES, 2, P], F32, name="hT", tag=bank, bufs=3 if bank == "new_ps" else 1)
             for g in range(PASSES):
                 for u in range(2):
                     nc.tensor.transpose(hT[:, g, u, :], h_words[:, 256 * g + u : 256 * (g + 1) : 2], ident_f32[:])
@@ -123,14 +125,14 @@ def tile_stackrnn_pb_kernel(
 
         def group_h(t):
             hT = part[t]
-            grouped = quant.tile([P, PASSES, P, 4], BF16, name="grouped", align_bytes=64)
+            grouped = quant.tile([P, PASSES, P, 4], BF16, name="grouped", align_bytes=64, bufs=3)
             nc.scalar.copy(out=grouped[:].bitcast(F32), in_=hT[:].rearrange("p g u b -> p g b u"))
             part[t] = grouped
 
         def quantise_h(t):
             grouped = part[t]
-            h_codes = quant.tile([P, PASSES, P], U32, name="h_codes", align_bytes=64, bufs=3)
-            h_scales = quant.tile([P, PASSES, P], U8, name="h_scales", align_bytes=64, bufs=3)
+            h_codes = quant.tile([P, PASSES, P], U32, name="h_codes", align_bytes=64, bufs=B_TILES)
+            h_scales = quant.tile([P, PASSES, P], U8, name="h_scales", align_bytes=64, bufs=B_TILES)
             nc.vector.quantize_mx(
                 out=h_codes[:].rearrange("p g b -> p (g b)").bitcast(FP8X4),
                 scales=h_scales[:].rearrange("p g b -> p (g b)"),
@@ -172,14 +174,14 @@ def tile_stackrnn_pb_kernel(
 
         def biased(t):
             logits = part[t]
-            logit_sb = soft.tile([P, 3, P], F32, name="logit_sb")
+            logit_sb = soft.tile([P, 3, P], F32, name="logit_sb", bufs=B_TILES)
             for a in range(3):
                 nc.scalar.activation(
                     out=logit_sb[:, a, :], in_=logits[:, a, :], func=FUNC.Identity, bias=bias_col[:, a : a + 1]
                 )
-            tanh_half = soft.tile([P, P], F32, name="tanh_half")
+            tanh_half = soft.tile([P, P], F32, name="tanh_half", bufs=B_TILES)
             nc.scalar.activation(out=tanh_half[:], in_=logits[:, 3, :], func=FUNC.Tanh, bias=half_bs[:], scale=0.5)
-            part[t] = (logits, logit_sb, tanh_half)
+            part[t] = (logit_sb, tanh_half)
 
         def store_out(t):
             out_ps = sums_of[t]
@@ -188,15 +190,11 @@ def tile_stackrnn_pb_kernel(
             nc.sync.dma_start(out=out_0[t * P : (t + 1) * P, :], in_=out_sb[:])
 
         def peak_of(t):
-            logits, logit_sb, tanh_half = part[t]
+            logit_sb, tanh_half = part[t]
             peak01 = soft.tile([P, P], F32, name="peak01")
-            nc.vector.scalar_tensor_tensor(
-                out=peak01[:], in0=logits[:, 0, :], scalar=bias_col[:, 0:1], in1=logit_sb[:, 1, :], op0=ALU.add, op1=ALU.max
-            )
+            nc.vector.tensor_max(out=peak01[:], in0=logit_sb[:, 0, :], in1=logit_sb[:, 1, :])
             peak = soft.tile([P, P], F32, name="peak")
-            nc.vector.scalar_tensor_tensor(
-                out=peak[:], in0=logits[:, 2, :], scalar=bias_col[:, 2:3], in1=peak01[:], op0=ALU.add, op1=ALU.max
-            )
+            nc.vector.tensor_max(out=peak[:], in0=peak01[:], in1=logit_sb[:, 2, :])
             part[t] = (logit_sb, tanh_half, peak)
 
         def shift(t, engine):
@@ -260,12 +258,12 @@ def tile_stackrnn_pb_kernel(
                 nc.scalar.copy(out=xT_sb[:], in_=xT[:])
                 turned[t, bank] = xT_sb
 
-        def multiply_vector(t, g):
-            first = (g % 2) * ROWS
-            shape = [P, 3, ROWS, P]
+        def multiply_vector(t, first_row, rows):
+            bank, first = divmod(first_row, BANK_ROWS)
+            shape = [P, 3, rows, P]
             nc.vector.tensor_tensor(
-                out=terms_of[t][:, :, g * ROWS : (g + 1) * ROWS, :],
-                in0=turned[t, g // 2][:, first : first + ROWS, :].unsqueeze(1).to_broadcast(shape),
+                out=terms_of[t][:, :, first_row : first_row + rows, :],
+                in0=turned[t, bank][:, first : first + rows, :].unsqueeze(1).to_broadcast(shape),
                 in1=made[t][0][:].unsqueeze(2).to_broadcast(shape),
                 op=ALU.mult,
             )
@@ -281,12 +279,12 @@ def tile_stackrnn_pb_kernel(
 
         pool_units = [(g, a) for g in range(VECTOR_GROUPS, GROUPS) for a in (POP, KEEP, PUSH)]
 
-        def back(t, g):
+        def back(t, g, alone=False):
             terms = terms_of[t]
             edges = made[t][1]
-            if g % 2 == 0:
-                staged[t] = stage.tile([P, 2 * ROWS, S], F32, name="new_sb")
-            new_sb = staged[t]
+            if (t, g // 2) not in staged:
+                staged[t, g // 2] = stage.tile([P, 2 * ROWS, S], F32, name="new_sb")
+            new_sb = staged[t, g // 2]
             new_ps = psum.tile([P, ROWS, S], F32, name="new_ps", tag="new_ps", bufs=3)
             for i in range(ROWS):
                 d = g * ROWS + i
@@ -302,38 +300,44 @@ def tile_stackrnn_pb_kernel(
                         start=(n == 0),
                         stop=(n == len(summands) - 1),
                     )
-            nc.scalar.copy(out=new_sb[:, (g % 2) * ROWS : (g % 2 + 1) * ROWS, :], in_=new_ps[:])
-            if g % 2 == 1:
+            half = slice((g % 2) * ROWS, (g % 2 + 1) * ROWS)
+            nc.scalar.copy(out=new_sb[:, half, :], in_=new_ps[:])
+            if alone:
+                nc.sync.dma_start(out=out_1[t * P : (t + 1) * P, g * ROWS : (g + 1) * ROWS, :], in_=new_sb[:, half, :])
+            elif g % 2 == 1:
                 nc.sync.dma_start(out=out_1[t * P : (t + 1) * P, (g - 1) * ROWS : (g + 1) * ROWS, :], in_=new_sb[:])
 
         ctx.enter_context(tc.manual_schedule())
-        turn_h(0)
+        turn_h(0, "new_ps")
+        turn_h(1, "new_ps")
         group_h(0)
         quantise_h(0)
         turn_biases()
         gate_matmuls(0)
-        turn_h(1)
-        biased(0)
         group_h(1)
-        forward(0, POOL_BANK)
+        quantise_h(1)
+        turn_h(2, "new_ps")
+        turn_h(3, "new_ps")
+        biased(0)
         peak_of(0)
         shift(0, nc.vector)
-        quantise_h(1)
+        gate_matmuls(1)
+        group_h(2)
         exponentials(0)
+        quantise_h(2)
+        group_h(3)
+        biased(1)
+        forward(0, POOL_BANK)
         forward(0, 0)
         forward(0, 1)
         total_of(0, nc.vector)
         invert(0)
         normalise(0, nc.vector)
         edge_rows(0, nc.vector)
-        gate_matmuls(1)
-        biased(1)
 
         for t in range(B_TILES):
             soon = t + 1 if t + 1 < B_TILES else None
-            later = t + 2 if t + 2 < B_TILES else None
             if t + AHEAD < B_TILES:
-                load_h(t + AHEAD, nc.sync)
                 load_x(t + AHEAD)
             terms_of[t] = term_pool.tile([P, 3, DEPTH, P], F32, name="terms")
             for j in range(VECTOR_GROUPS):
@@ -341,8 +345,20 @@ def tile_stackrnn_pb_kernel(
                     forward(t, 2)
                 if soon is not None and j in (2, 3, 4):
                     forward(soon, (POOL_BANK, 0, 1)[j - 2])
-                multiply_vector(t, j)
+                if soon is None and j == VECTOR_GROUPS - 1:
+                    multiply_vector(t, j * ROWS, ROWS // 2)
+                    multiply_vector(t, j * ROWS + ROWS // 2, ROWS // 2)
+                else:
+                    multiply_vector(t, j * ROWS, ROWS)
                 multiply_pool(t, *pool_units[j])
+                if t == 0:
+                    if j + 4 < B_TILES:
+                        turn_h(j + 4, "bank_a")
+                        group_h(j + 4)
+                    gate_matmuls(j + 2)
+                    biased(j + 2)
+                    if j + 3 < B_TILES:
+                        quantise_h(j + 3)
                 if j == 0:
                     if soon is not None:
                         peak_of(soon)
@@ -352,36 +368,28 @@ def tile_stackrnn_pb_kernel(
                 if j == 1:
                     if soon is not None:
                         shift(soon, nc.gpsimd)
-                    if later is not None:
-                        turn_h(later)
                     if t > 0:
                         back(t - 1, 6)
                     if soon is not None:
                         exponentials(soon)
                     if t > 0:
                         back(t - 1, 7)
-                    if later is not None:
-                        group_h(later)
                 if j == 2:
                     if soon is not None:
                         total_of(soon, nc.gpsimd)
                 if j == 3:
-                    if later is not None:
-                        quantise_h(later)
                     if soon is not None:
                         invert(soon)
                         normalise(soon, nc.gpsimd)
                 if j == 4:
-                    if later is not None:
-                        gate_matmuls(later)
                     out_matmuls(t)
+                if soon is None and j == VECTOR_GROUPS - 1:
+                    back(t, GROUPS - 1, alone=True)
                 if j >= 2:
                     back(t, j - 2)
                 if j == 5:
                     if soon is not None:
                         edge_rows(soon, nc.gpsimd)
-                    if later is not None:
-                        biased(later)
                     store_out(t)
-        for g in range(VECTOR_GROUPS - 2, GROUPS):
-            back(B_TILES - 1, g)
+        for g in range(VECTOR_GROUPS - 2, GROUPS - 1):
+            back(B_TILES - 1, g, alone=True)

@@ -29,7 +29,7 @@ BANK_ROWS = 2 * ROWS
 BANKS = DEPTH // BANK_ROWS
 POOL_BANK = BANKS - 1
 VECTOR_GROUPS = GROUPS - 2
-COUNTED_GROUPS = (0, 1, 3, 4, 6)
+COUNTED_GROUPS = (0, 4, 6)
 AHEAD = 4
 
 FLOPS = 2 * BATCH * K * (N_GATES + N_OUT)
@@ -191,10 +191,10 @@ def tile_stackrnn_pb_kernel(
 
         def peak_of(t):
             logit_sb, tanh_half = part[t]
-            peak01 = soft.tile([P, P], F32, name="peak01")
-            nc.vector.tensor_max(out=peak01[:], in0=logit_sb[:, 0, :], in1=logit_sb[:, 1, :])
             peak = soft.tile([P, P], F32, name="peak")
-            nc.vector.tensor_max(out=peak[:], in0=peak01[:], in1=logit_sb[:, 2, :])
+            nc.vector.tensor_reduce(
+                out=peak[:], in_=logit_sb[:].rearrange("p a b -> p b a"), axis=mybir.AxisListType.X, op=ALU.max
+            )
             part[t] = (logit_sb, tanh_half, peak)
 
         def shift(t, engine):
@@ -268,16 +268,15 @@ def tile_stackrnn_pb_kernel(
                 op=ALU.mult,
             )
 
-        def multiply_pool(t, g, a):
-            first = (g % 2) * ROWS
+        def multiply_pool(t, a):
+            rows = BANK_ROWS - 1 if a == PUSH else BANK_ROWS
+            first = POOL_BANK * BANK_ROWS
             nc.gpsimd.tensor_tensor(
-                out=terms_of[t][:, a, g * ROWS : (g + 1) * ROWS, :],
-                in0=turned[t, g // 2][:, first : first + ROWS, :],
-                in1=made[t][0][:, a, :].unsqueeze(1).to_broadcast([P, ROWS, P]),
+                out=terms_of[t][:, a, first : first + rows, :],
+                in0=turned[t, POOL_BANK][:, 0:rows, :],
+                in1=made[t][0][:, a, :].unsqueeze(1).to_broadcast([P, rows, P]),
                 op=ALU.mult,
             )
-
-        pool_units = [(g, a) for g in range(VECTOR_GROUPS, GROUPS) for a in (POP, KEEP, PUSH)]
 
         def back(t, g, alone=False):
             terms = terms_of[t]
@@ -350,7 +349,8 @@ def tile_stackrnn_pb_kernel(
                     multiply_vector(t, j * ROWS + ROWS // 2, ROWS // 2)
                 else:
                     multiply_vector(t, j * ROWS, ROWS)
-                multiply_pool(t, *pool_units[j])
+                if j % 2 == 0:
+                    multiply_pool(t, (POP, KEEP, PUSH)[j // 2])
                 if t == 0:
                     if j + 4 < B_TILES:
                         turn_h(j + 4, "bank_a")

@@ -340,10 +340,10 @@ def tile_stackrnn_pb_kernel(
                 load_x(t + AHEAD)
             terms_of[t] = term_pool.tile([P, 3, DEPTH, P], F32, name="terms")
             for j in range(VECTOR_GROUPS):
-                if j == 0:
+                if j == 1:
                     forward(t, 2)
-                if soon is not None and j in (2, 3, 4):
-                    forward(soon, (POOL_BANK, 0, 1)[j - 2])
+                if soon is not None and j in (3, 4, 5):
+                    forward(soon, (POOL_BANK, 0, 1)[j - 3])
                 if soon is None and j == VECTOR_GROUPS - 1:
                     multiply_vector(t, j * ROWS, ROWS // 2)
                     multiply_vector(t, j * ROWS + ROWS // 2, ROWS // 2)

@@ -22,15 +22,17 @@ DEPTH = 32
 N_OUT = 512
 N_GATES = 4 * S
 B_TILES = BATCH // P
-PUSH, POP, KEEP = 0, 1, 2
+PUSH, POP, KEEP, TOP = 0, 1, 2, 3
+BATCHES = ((0,), (1,), (2, 3), (4, 5), (6, 7))
+BATCH_OF = {t: batch for batch in BATCHES for t in batch}
 ROWS = 4
 GROUPS = DEPTH // ROWS
 BANK_ROWS = 2 * ROWS
 BANKS = DEPTH // BANK_ROWS
 POOL_BANK = BANKS - 1
-VECTOR_GROUPS = GROUPS - 2
+STEPS = GROUPS - 2
 COUNTED_GROUPS = (0, 4, 6)
-AHEAD = 4
+AHEAD = 3
 
 FLOPS = 2 * BATCH * K * (N_GATES + N_OUT)
 
@@ -42,9 +44,9 @@ def tile_stackrnn_pb_kernel(
     with ExitStack() as ctx:
         const = ctx.enter_context(tc.tile_pool(name="const", bufs=1))
         loads = ctx.enter_context(tc.tile_pool(name="loads", bufs=AHEAD + 1))
-        quant = ctx.enter_context(tc.tile_pool(name="quant", bufs=2))
-        soft = ctx.enter_context(tc.tile_pool(name="soft", bufs=2))
-        gate_pool = ctx.enter_context(tc.tile_pool(name="gates", bufs=3))
+        quant = ctx.enter_context(tc.tile_pool(name="quant", bufs=3))
+        soft = ctx.enter_context(tc.tile_pool(name="soft", bufs=1))
+        gate_pool = ctx.enter_context(tc.tile_pool(name="gates", bufs=2))
         term_pool = ctx.enter_context(tc.tile_pool(name="terms", bufs=2))
         stage = ctx.enter_context(tc.tile_pool(name="stage", bufs=4))
         psum = ctx.enter_context(tc.psum_pool(name="psum", bufs=1))
@@ -52,15 +54,22 @@ def tile_stackrnn_pb_kernel(
         h_of, x_of = {}, {}
 
         def load_h(t, queue):
-            h_of[t] = loads.tile([P, K], BF16, name="h_sb", bufs=B_TILES // 2)
+            h_of[t] = loads.tile([P, K], BF16, name="h_sb", bufs=5)
             queue.dma_start(out=h_of[t][:], in_=h[t * P : (t + 1) * P, :])
 
         def load_x(t):
             x_of[t] = loads.tile([P, DEPTH, S], BF16, name="x_sb")
             nc.sync.dma_start(out=x_of[t][:], in_=stack[t * P : (t + 1) * P, :, :])
 
+        bias_rows = const.tile([P, P], BF16, name="bias_rows")
+        nc.vector.memset(bias_rows[:].bitcast(I32), 0)
+        w_codes = const.tile([P, PASSES, N_GATES + N_OUT], U32, name="w_codes", align_bytes=64)
+        w_scales = const.tile([P, PASSES, N_GATES + N_OUT], U8, name="w_scales", align_bytes=64)
+        nc.vector.memset(w_scales[:].bitcast(I32), 0)
+
         load_h(0, nc.scalar)
-        load_h(1, nc.scalar)
+        nc.scalar.dma_start(out=bias_rows[0:3, :], in_=ba.rearrange("(a s) -> a s", a=3))
+        nc.scalar.dma_start(out=bias_rows[3:4, :], in_=bs.rearrange("(a s) -> a s", a=1))
 
         ident_f32 = const.tile([P, P], F32, name="ident_f32")
         make_identity(nc, ident_f32[:])
@@ -69,37 +78,31 @@ def tile_stackrnn_pb_kernel(
         warm = const.tile([P, 1], F32, name="warm")
         nc.scalar.activation(out=warm[:], in_=ident_f32[:, 0:1], func=FUNC.Exp)
 
-        w_codes = const.tile([P, PASSES, N_GATES + N_OUT], U32, name="w_codes", align_bytes=64)
-        w_scales = const.tile([P, PASSES, N_GATES + N_OUT], U8, name="w_scales", align_bytes=64)
-        nc.vector.memset(w_scales[:].bitcast(I32), 0)
-        bias_rows = const.tile([P, P], BF16, name="bias_rows")
-        nc.vector.memset(bias_rows[:].bitcast(I32), 0)
-
-        def load_weights(weights):
-            for words, scales, first, width in weights:
-                for quad in range(4):
-                    nc.sync.dma_start(
-                        out=w_scales[32 * quad : 32 * quad + 4, :, first : first + width].bitcast(I32),
-                        in_=scales[:, 4 * quad : 4 * quad + 4, :].rearrange("g r n -> r g n").bitcast(I32),
-                    )
-            for words, scales, first, width in weights:
+        def load_weights(words, scales, first, width):
+            for quad in range(4):
                 nc.sync.dma_start(
-                    out=w_codes[:, :, first : first + width].bitcast(I32),
-                    in_=words.rearrange("g p n t -> p g (n t)").bitcast(I32),
+                    out=w_scales[32 * quad : 32 * quad + 4, :, first : first + width].bitcast(I32),
+                    in_=scales[:, 4 * quad : 4 * quad + 4, :].rearrange("g r n -> r g n").bitcast(I32),
                 )
+            nc.sync.dma_start(
+                out=w_codes[:, :, first : first + width].bitcast(I32),
+                in_=words.rearrange("g p n t -> p g (n t)").bitcast(I32),
+            )
 
-        load_weights(((Wa_words, Wa_scales, 0, 3 * S), (Ws_words, Ws_scales, 3 * S, S)))
-        nc.scalar.dma_start(out=bias_rows[0:3, :], in_=ba.rearrange("(a s) -> a s", a=3))
-        nc.scalar.dma_start(out=bias_rows[3:4, :], in_=bs.rearrange("(a s) -> a s", a=1))
+        load_weights(Wa_words, Wa_scales, 0, 3 * S)
+        load_h(1, nc.sync)
         load_h(2, nc.sync)
-        load_h(3, nc.sync)
         load_x(0)
-        load_weights(((Wo_words, Wo_scales, N_GATES, N_OUT),))
+        load_weights(Ws_words, Ws_scales, 3 * S, S)
+        load_h(3, nc.sync)
+        load_h(4, nc.sync)
+        load_x(1)
+        for t in range(5, B_TILES):
+            load_h(t, nc.sync)
+        load_weights(Wo_words, Wo_scales, N_GATES, N_OUT)
         bo_all = const.tile([P, N_OUT], BF16, name="bo_all")
         nc.sync.dma_start(out=bo_all[:], in_=bo.partition_broadcast(P))
-        for t in range(4, B_TILES):
-            load_h(t, nc.sync)
-        for t in range(1, AHEAD):
+        for t in range(2, AHEAD):
             load_x(t)
         bias_col = const.tile([P, 4], F32, name="bias_col")
         half_bs = const.tile([P, 1], F32, name="half_bs")
@@ -110,44 +113,43 @@ def tile_stackrnn_pb_kernel(
             nc.vector.tensor_copy(out=bias_col[:], in_=bias_ps[:, 0:4])
             nc.vector.tensor_scalar_mul(out=half_bs[:], in0=bias_col[:, 3:4], scalar1=0.5)
 
-        over_actions = [P, 3, P]
-        part = {}
+        turned_h, grouped_h = {}, {}
         codes_of = {}
-        sums_of = {}
+        logits_of = {}
+        sums_of, out_of = {}, {}
 
-        def turn_h(t, bank):
+        def turn_h(t):
             h_words = h_of[t][:].bitcast(F32)
-            hT = psum.tile([P, PASSES, 2, P], F32, name="hT", tag=bank, bufs=3 if bank == "new_ps" else 1)
+            hT = psum.tile([P, PASSES, 2, P], F32, name="hT", tag="new_ps", bufs=3)
             for g in range(PASSES):
                 for u in range(2):
                     nc.tensor.transpose(hT[:, g, u, :], h_words[:, 256 * g + u : 256 * (g + 1) : 2], ident_f32[:])
-            part[t] = hT
+            turned_h[t] = hT
 
         def group_h(t):
-            hT = part[t]
-            grouped = quant.tile([P, PASSES, P, 4], BF16, name="grouped", align_bytes=64, bufs=3)
-            nc.scalar.copy(out=grouped[:].bitcast(F32), in_=hT[:].rearrange("p g u b -> p g b u"))
-            part[t] = grouped
+            grouped = quant.tile([P, PASSES, P, 4], BF16, name="grouped", align_bytes=64)
+            nc.scalar.copy(out=grouped[:].bitcast(F32), in_=turned_h[t][:].rearrange("p g u b -> p g b u"))
+            grouped_h[t] = grouped
 
         def quantise_h(t):
-            grouped = part[t]
             h_codes = quant.tile([P, PASSES, P], U32, name="h_codes", align_bytes=64, bufs=B_TILES)
             h_scales = quant.tile([P, PASSES, P], U8, name="h_scales", align_bytes=64, bufs=B_TILES)
             nc.vector.quantize_mx(
                 out=h_codes[:].rearrange("p g b -> p (g b)").bitcast(FP8X4),
                 scales=h_scales[:].rearrange("p g b -> p (g b)"),
-                in_=grouped[:].rearrange("p g b t -> p (g b t)"),
+                in_=grouped_h[t][:].rearrange("p g b t -> p (g b t)"),
             )
             codes_of[t] = (h_codes, h_scales)
 
-        def gate_matmuls(t):
+        def gate_matmuls(t, gates=(PUSH, POP, KEEP, TOP)):
             h_codes, h_scales = codes_of[t]
-            logits = psum.tile([P, 4, P], F32, name="logits", tag="bank_b")
-            for j in range(4):
+            if t not in logits_of:
+                logits_of[t] = psum.tile([P, 4, P], F32, name="logits", tag="bank_a" if t == 0 else "bank_b")
+            for j in gates:
                 cols = slice(j * S, (j + 1) * S)
                 for g in range(PASSES):
                     nc.tensor.matmul_mx(
-                        out=logits[:, j, :],
+                        out=logits_of[t][:, j, :],
                         lhsT=w_codes[:, g, cols].bitcast(FP8X4),
                         lhsT_scale=w_scales[:, g, cols],
                         rhs=h_codes[:, g, :].bitcast(FP8X4),
@@ -155,7 +157,6 @@ def tile_stackrnn_pb_kernel(
                         start=(g == 0),
                         stop=(g == PASSES - 1),
                     )
-            part[t] = logits
 
         def out_matmuls(t):
             h_codes, h_scales = codes_of[t]
@@ -170,79 +171,101 @@ def tile_stackrnn_pb_kernel(
                     start=(g == 0),
                     stop=(g == PASSES - 1),
                 )
-            sums_of[t] = out_ps
-
-        def biased(t):
-            logits = part[t]
-            logit_sb = soft.tile([P, 3, P], F32, name="logit_sb", bufs=B_TILES)
-            for a in range(3):
-                nc.scalar.activation(
-                    out=logit_sb[:, a, :], in_=logits[:, a, :], func=FUNC.Identity, bias=bias_col[:, a : a + 1]
-                )
-            tanh_half = soft.tile([P, P], F32, name="tanh_half", bufs=B_TILES)
-            nc.scalar.activation(out=tanh_half[:], in_=logits[:, 3, :], func=FUNC.Tanh, bias=half_bs[:], scale=0.5)
-            part[t] = (logit_sb, tanh_half)
+            out_sb = stage.tile([P, N_OUT], F32, name="out_sb", bufs=2)
+            nc.scalar.copy(out=out_sb[:], in_=out_ps[:])
+            out_of[t] = out_sb
 
         def store_out(t):
-            out_ps = sums_of[t]
-            out_sb = stage.tile([P, N_OUT], F32, name="out_sb", bufs=2)
-            nc.vector.tensor_add(out=out_sb[:], in0=out_ps[:], in1=bo_all[:])
+            out_sb = out_of[t]
+            nc.gpsimd.tensor_tensor(out=out_sb[:], in0=out_sb[:], in1=bo_all[:], op=ALU.add)
             nc.sync.dma_start(out=out_0[t * P : (t + 1) * P, :], in_=out_sb[:])
 
-        def peak_of(t):
-            logit_sb, tanh_half = part[t]
-            peak = soft.tile([P, P], F32, name="peak")
+        logit_sb, tanh_half, top, peak, shifted, expo, total, inverse = {}, {}, {}, {}, {}, {}, {}, {}
+        gates_of, edges_of, edge_tile, gate_tile = {}, {}, {}, {}
+
+        def over_actions(tile, n):
+            return tile[:].unsqueeze(2).to_broadcast([P, n, 3, P])
+
+        def biased(t):
+            batch = BATCH_OF[t]
+            n, i = len(batch), batch.index(t)
+            if i == 0:
+                logit_sb[batch] = soft.tile([P, n, 3, P], F32, name="logit_sb", bufs=4)
+                tanh_half[batch] = soft.tile([P, n, P], F32, name="tanh_half", bufs=4)
+            for a in range(3):
+                nc.scalar.activation(
+                    out=logit_sb[batch][:, i, a, :],
+                    in_=logits_of[t][:, a, :],
+                    func=FUNC.Identity,
+                    bias=bias_col[:, a : a + 1],
+                )
+
+        def squashed(t):
+            batch = BATCH_OF[t]
+            nc.scalar.activation(
+                out=tanh_half[batch][:, batch.index(t), :],
+                in_=logits_of[t][:, TOP, :],
+                func=FUNC.Tanh,
+                bias=half_bs[:],
+                scale=0.5,
+            )
+
+        def peak_of(batch):
+            n = len(batch)
+            peak[batch] = soft.tile([P, n, P], F32, name="peak")
             nc.vector.tensor_reduce(
-                out=peak[:], in_=logit_sb[:].rearrange("p a b -> p b a"), axis=mybir.AxisListType.X, op=ALU.max
+                out=peak[batch][:],
+                in_=logit_sb[batch][:].rearrange("p n a b -> p n b a"),
+                axis=mybir.AxisListType.X,
+                op=ALU.max,
             )
-            part[t] = (logit_sb, tanh_half, peak)
 
-        def shift(t, engine):
-            logit_sb, tanh_half, peak = part[t]
-            shifted = soft.tile([P, 3, P], F32, name="shifted")
+        def shift(batch, engine):
+            n = len(batch)
+            shifted[batch] = soft.tile([P, n, 3, P], F32, name="shifted")
             engine.tensor_tensor(
-                out=shifted[:], in0=logit_sb[:], in1=peak[:].unsqueeze(1).to_broadcast(over_actions), op=ALU.subtract
+                out=shifted[batch][:], in0=logit_sb[batch][:], in1=over_actions(peak[batch], n), op=ALU.subtract
             )
-            part[t] = (tanh_half, shifted)
 
-        def exponentials(t):
-            tanh_half, shifted = part[t]
-            expo = soft.tile([P, 3, P], F32, name="expo")
-            nc.scalar.activation(out=expo[:], in_=shifted[:], func=FUNC.Exp)
-            top = soft.tile([P, P], F32, name="top")
-            nc.scalar.activation(out=top[:], in_=tanh_half[:], func=FUNC.Copy, bias=0.5, scale=0.5)
-            part[t] = (top, expo)
+        def exponentials(batch):
+            n = len(batch)
+            expo[batch] = soft.tile([P, n, 3, P], F32, name="expo", bufs=2)
+            nc.scalar.activation(out=expo[batch][:], in_=shifted[batch][:], func=FUNC.Exp)
 
-        def total_of(t, engine):
-            top, expo = part[t]
-            total01 = soft.tile([P, P], F32, name="total01")
-            engine.tensor_tensor(out=total01[:], in0=expo[:, 0, :], in1=expo[:, 1, :], op=ALU.add)
-            total = soft.tile([P, P], F32, name="total")
-            engine.tensor_tensor(out=total[:], in0=total01[:], in1=expo[:, 2, :], op=ALU.add)
-            part[t] = (top, expo, total)
+        def top_row(batch):
+            n = len(batch)
+            top[batch] = soft.tile([P, n, P], F32, name="top", bufs=2)
+            nc.scalar.activation(out=top[batch][:], in_=tanh_half[batch][:], func=FUNC.Copy, bias=0.5, scale=0.5)
 
-        def invert(t):
-            top, expo, total = part[t]
-            inverse = soft.tile([P, P], F32, name="inverse")
-            nc.vector.reciprocal(out=inverse[:], in_=total[:])
-            part[t] = (top, expo, inverse)
+        def total_of(batch, engine):
+            n = len(batch)
+            total01 = soft.tile([P, n, P], F32, name="total01")
+            engine.tensor_tensor(out=total01[:], in0=expo[batch][:, :, 0, :], in1=expo[batch][:, :, 1, :], op=ALU.add)
+            total[batch] = soft.tile([P, n, P], F32, name="total")
+            engine.tensor_tensor(out=total[batch][:], in0=total01[:], in1=expo[batch][:, :, 2, :], op=ALU.add)
 
-        made = {}
+        def invert(batch):
+            n = len(batch)
+            inverse[batch] = soft.tile([P, n, P], F32, name="inverse")
+            nc.vector.reciprocal(out=inverse[batch][:], in_=total[batch][:])
 
-        def normalise(t, engine):
-            top, expo, inverse = part[t]
-            gates = gate_pool.tile([P, 3, P], F32, name="gates")
-            engine.tensor_tensor(
-                out=gates[:], in0=expo[:], in1=inverse[:].unsqueeze(1).to_broadcast(over_actions), op=ALU.mult
+        def normalise(batch, engine):
+            n = len(batch)
+            gates = gate_pool.tile([P, n, 3, P], F32, name="gates")
+            engine.tensor_tensor(out=gates[:], in0=expo[batch][:], in1=over_actions(inverse[batch], n), op=ALU.mult)
+            edges = gate_pool.tile([P, n, 2, P], F32, name="edges")
+            gate_tile[batch], edge_tile[batch] = gates, edges
+            for i, t in enumerate(batch):
+                gates_of[t] = gates[:, i, :, :]
+                edges_of[t] = edges[:, i, :, :]
+
+        def push_edge(batch):
+            nc.gpsimd.tensor_tensor(
+                out=edge_tile[batch][:, :, 0, :], in0=gate_tile[batch][:, :, PUSH, :], in1=top[batch][:], op=ALU.mult
             )
-            part[t] = (top, gates)
 
-        def edge_rows(t, engine):
-            top, gates = part[t]
-            edges = gate_pool.tile([P, 2, P], F32, name="edges")
-            engine.tensor_tensor(out=edges[:, 0, :], in0=gates[:, PUSH, :], in1=top[:], op=ALU.mult)
-            nc.scalar.mul(out=edges[:, 1, :], in_=gates[:, POP, :], mul=-1.0)
-            made[t] = (gates, edges)
+        def pop_edge(batch):
+            nc.scalar.mul(out=edge_tile[batch][:, :, 1, :], in_=gate_tile[batch][:, :, POP, :], mul=-1.0)
 
         turned = {}
         terms_of = {}
@@ -264,7 +287,7 @@ def tile_stackrnn_pb_kernel(
             nc.vector.tensor_tensor(
                 out=terms_of[t][:, :, first_row : first_row + rows, :],
                 in0=turned[t, bank][:, first : first + rows, :].unsqueeze(1).to_broadcast(shape),
-                in1=made[t][0][:].unsqueeze(2).to_broadcast(shape),
+                in1=gates_of[t].unsqueeze(2).to_broadcast(shape),
                 op=ALU.mult,
             )
 
@@ -274,13 +297,12 @@ def tile_stackrnn_pb_kernel(
             nc.gpsimd.tensor_tensor(
                 out=terms_of[t][:, a, first : first + rows, :],
                 in0=turned[t, POOL_BANK][:, 0:rows, :],
-                in1=made[t][0][:, a, :].unsqueeze(1).to_broadcast([P, rows, P]),
+                in1=gates_of[t][:, a, :].unsqueeze(1).to_broadcast([P, rows, P]),
                 op=ALU.mult,
             )
 
         def back(t, g, alone=False):
-            terms = terms_of[t]
-            edges = made[t][1]
+            terms, edges = terms_of[t], edges_of[t]
             if (t, g // 2) not in staged:
                 staged[t, g // 2] = stage.tile([P, 2 * ROWS, S], F32, name="new_sb")
             new_sb = staged[t, g // 2]
@@ -307,89 +329,130 @@ def tile_stackrnn_pb_kernel(
                 nc.sync.dma_start(out=out_1[t * P : (t + 1) * P, (g - 1) * ROWS : (g + 1) * ROWS, :], in_=new_sb[:])
 
         ctx.enter_context(tc.manual_schedule())
-        turn_h(0, "new_ps")
-        turn_h(1, "new_ps")
+        turn_h(0)
         group_h(0)
         quantise_h(0)
         turn_biases()
-        gate_matmuls(0)
-        group_h(1)
-        quantise_h(1)
-        turn_h(2, "new_ps")
-        turn_h(3, "new_ps")
+        gate_matmuls(0, (PUSH, POP, KEEP))
         biased(0)
-        peak_of(0)
-        shift(0, nc.vector)
-        gate_matmuls(1)
-        group_h(2)
-        exponentials(0)
-        quantise_h(2)
-        group_h(3)
+        turn_h(1)
+        group_h(1)
+        peak_of((0,))
+        shift((0,), nc.vector)
+        exponentials((0,))
+        quantise_h(1)
+        turn_h(2)
+        gate_matmuls(1, (PUSH, POP, KEEP))
         biased(1)
-        forward(0, POOL_BANK)
         forward(0, 0)
+        forward(0, POOL_BANK)
+        total_of((0,), nc.vector)
+        invert((0,))
+        normalise((0,), nc.vector)
+        peak_of((1,))
+        shift((1,), nc.gpsimd)
+        gate_matmuls(0, (TOP,))
+        squashed(0)
+        top_row((0,))
+        group_h(2)
+        gate_matmuls(1, (TOP,))
         forward(0, 1)
-        total_of(0, nc.vector)
-        invert(0)
-        normalise(0, nc.vector)
-        edge_rows(0, nc.vector)
+        turn_h(3)
+        push_edge((0,))
+        pop_edge((0,))
+        squashed(1)
+        exponentials((1,))
+        top_row((1,))
 
         for t in range(B_TILES):
-            soon = t + 1 if t + 1 < B_TILES else None
+            last = t + 1 == B_TILES
+            begun = {0: (2, 3), 2: (4, 5), 4: (6, 7)}.get(t)
+            finished = {0: (1,), 1: (2, 3), 3: (4, 5), 5: (6, 7)}.get(t)
             if t + AHEAD < B_TILES:
                 load_x(t + AHEAD)
             terms_of[t] = term_pool.tile([P, 3, DEPTH, P], F32, name="terms")
-            for j in range(VECTOR_GROUPS):
+            for j in range(STEPS):
                 if j == 1:
                     forward(t, 2)
-                if soon is not None and j in (3, 4, 5):
-                    forward(soon, (POOL_BANK, 0, 1)[j - 3])
-                if soon is None and j == VECTOR_GROUPS - 1:
+                if not last and j in (2, 4, 5):
+                    forward(t + 1, {2: POOL_BANK, 4: 0, 5: 1}[j])
+                if last and j == STEPS - 1:
                     multiply_vector(t, j * ROWS, ROWS // 2)
                     multiply_vector(t, j * ROWS + ROWS // 2, ROWS // 2)
                 else:
                     multiply_vector(t, j * ROWS, ROWS)
-                if j % 2 == 0:
-                    multiply_pool(t, (POP, KEEP, PUSH)[j // 2])
-                if t == 0:
-                    if j + 4 < B_TILES:
-                        turn_h(j + 4, "bank_a")
-                        group_h(j + 4)
-                    gate_matmuls(j + 2)
-                    biased(j + 2)
-                    if j + 3 < B_TILES:
-                        quantise_h(j + 3)
+
                 if j == 0:
-                    if soon is not None:
-                        peak_of(soon)
-                    if t > 0:
-                        back(t - 1, 4)
-                        back(t - 1, 5)
+                    multiply_pool(t, POP)
+                    if t in (3, 5):
+                        total_of(finished, nc.gpsimd)
                 if j == 1:
-                    if soon is not None:
-                        shift(soon, nc.gpsimd)
-                    if t > 0:
-                        back(t - 1, 6)
-                    if soon is not None:
-                        exponentials(soon)
-                    if t > 0:
-                        back(t - 1, 7)
+                    if t in (0, 1):
+                        total_of(finished, nc.gpsimd)
+                    if t in (2, 4):
+                        shift(begun, nc.gpsimd)
+                    if t > 1:
+                        store_out(t - 1)
                 if j == 2:
-                    if soon is not None:
-                        total_of(soon, nc.gpsimd)
-                if j == 3:
-                    if soon is not None:
-                        invert(soon)
-                        normalise(soon, nc.gpsimd)
+                    multiply_pool(t, KEEP)
+                if j == 3 and t in (0, 1):
+                    normalise(finished, nc.gpsimd)
                 if j == 4:
+                    if t == 1:
+                        store_out(0)
+                    if t in (3, 5):
+                        normalise(finished, nc.gpsimd)
+                    multiply_pool(t, PUSH)
+                if j == 5:
+                    if finished is not None:
+                        push_edge(finished)
+                    if t == 0:
+                        shift(begun, nc.gpsimd)
+                    if last:
+                        store_out(t)
+
+                if t == 1 and j == 0:
+                    exponentials(finished)
+                    top_row(finished)
+                if t > 0 and j == 0:
+                    back(t - 1, 4)
+                    back(t - 1, 5)
+                if t > 0 and j == 1:
+                    back(t - 1, 6)
+                    back(t - 1, 7)
+
+                if begun is not None and j == (3 if t == 0 else 0):
+                    peak_of(begun)
+                if finished is not None and j == (2 if t < 2 else 3):
+                    invert(finished)
+                if finished is not None and j == (4 if t == 0 else 5):
+                    pop_edge(finished)
+                if t in (2, 4) and j == 5:
+                    exponentials(begun)
+                    top_row(begun)
+
+                if t == 1 and j == 1:
+                    out_matmuls(0)
+                if t > 0 and j == (1 if last else 4):
                     out_matmuls(t)
-                if soon is None and j == VECTOR_GROUPS - 1:
+                if last and j == STEPS - 1:
                     back(t, GROUPS - 1, alone=True)
                 if j >= 2:
                     back(t, j - 2)
-                if j == 5:
-                    if soon is not None:
-                        edge_rows(soon, nc.gpsimd)
-                    store_out(t)
-        for g in range(VECTOR_GROUPS - 2, GROUPS - 1):
+
+                if t == 0:
+                    if j + 3 < B_TILES:
+                        group_h(j + 3)
+                    if j > 0:
+                        gate_matmuls(j + 1)
+                        biased(j + 1)
+                        squashed(j + 1)
+                    if j + 4 < B_TILES:
+                        turn_h(j + 4)
+                    quantise_h(j + 2)
+                if t == 1 and j == 0:
+                    gate_matmuls(B_TILES - 1)
+                    biased(B_TILES - 1)
+                    squashed(B_TILES - 1)
+        for g in range(STEPS - 2, GROUPS - 1):
             back(B_TILES - 1, g, alone=True)

@@ -31,7 +31,7 @@ BANK_ROWS = 2 * ROWS
 BANKS = DEPTH // BANK_ROWS
 POOL_BANK = BANKS - 1
 STEPS = GROUPS - 2
-COUNTED_GROUPS = (0, 4, 6)
+COUNTED_ROWS = (0, 4 * ROWS, 6 * ROWS)
 AHEAD = 3
 
 FLOPS = 2 * BATCH * K * (N_GATES + N_OUT)
@@ -120,15 +120,28 @@ def tile_stackrnn_pb_kernel(
 
         def turn_h(t):
             h_words = h_of[t][:].bitcast(F32)
-            hT = psum.tile([P, PASSES, 2, P], F32, name="hT", tag="new_ps", bufs=3)
+            if t == 0:
+                turned_h[t] = []
+                for g in range(PASSES):
+                    hT = psum.tile([P, 2, P], F32, name="hT", tag="new_ps", bufs=3)
+                    turned_h[t].append(hT[:])
+            else:
+                hT = psum.tile([P, PASSES, 2, P], F32, name="hT", tag="new_ps", bufs=3)
+                turned_h[t] = [hT[:, g, :, :] for g in range(PASSES)]
             for g in range(PASSES):
                 for u in range(2):
-                    nc.tensor.transpose(hT[:, g, u, :], h_words[:, 256 * g + u : 256 * (g + 1) : 2], ident_f32[:])
-            turned_h[t] = hT
+                    words = h_words[:, 256 * g + u : 256 * (g + 1) : 2]
+                    nc.tensor.transpose(turned_h[t][g][:, u, :], words, ident_f32[:])
+            if t > 0:
+                turned_h[t] = hT
 
         def group_h(t):
             grouped = quant.tile([P, PASSES, P, 4], BF16, name="grouped", align_bytes=64)
-            nc.scalar.copy(out=grouped[:].bitcast(F32), in_=turned_h[t][:].rearrange("p g u b -> p g b u"))
+            if t == 0:
+                for g, copy in enumerate((nc.scalar.copy, nc.vector.tensor_copy)):
+                    copy(out=grouped[:, g, :, :].bitcast(F32), in_=turned_h[t][g].rearrange("p u b -> p b u"))
+            else:
+                nc.scalar.copy(out=grouped[:].bitcast(F32), in_=turned_h[t][:].rearrange("p g u b -> p g b u"))
             grouped_h[t] = grouped
 
         def quantise_h(t):
@@ -301,14 +314,25 @@ def tile_stackrnn_pb_kernel(
                 op=ALU.mult,
             )
 
-        def back(t, g, alone=False):
-            terms, edges = terms_of[t], edges_of[t]
+        def back(t, g, parts=0):
             if (t, g // 2) not in staged:
                 staged[t, g // 2] = stage.tile([P, 2 * ROWS, S], F32, name="new_sb")
             new_sb = staged[t, g // 2]
-            new_ps = psum.tile([P, ROWS, S], F32, name="new_ps", tag="new_ps", bufs=3)
-            for i in range(ROWS):
-                d = g * ROWS + i
+            rows = ROWS // max(parts, 1)
+            for first in range(0, ROWS, rows):
+                at = slice((g % 2) * ROWS + first, (g % 2) * ROWS + first + rows)
+                add_rows(t, g * ROWS + first, rows, new_sb[:, at, :])
+                if parts:
+                    d = g * ROWS + first
+                    nc.sync.dma_start(out=out_1[t * P : (t + 1) * P, d : d + rows, :], in_=new_sb[:, at, :])
+            if g % 2 == 1 and not parts:
+                nc.sync.dma_start(out=out_1[t * P : (t + 1) * P, (g - 1) * ROWS : (g + 1) * ROWS, :], in_=new_sb[:])
+
+        def add_rows(t, first, rows, new_sb):
+            terms, edges = terms_of[t], edges_of[t]
+            new_ps = psum.tile([P, rows, S], F32, name="new_ps", tag="new_ps", bufs=3)
+            for i in range(rows):
+                d = first + i
                 pushed = edges[:, 0, :] if d == 0 else terms[:, PUSH, d - 1, :]
                 popped = edges[:, 1, :] if d == DEPTH - 1 else terms[:, POP, d + 1, :]
                 summands = (pushed, terms[:, KEEP, d, :], popped)
@@ -317,22 +341,17 @@ def tile_stackrnn_pb_kernel(
                         out=new_ps[:, i, :],
                         lhsT=term,
                         rhs=ident_f32[:],
-                        is_transpose=not (g in COUNTED_GROUPS and i == 0 and n == 0),
+                        is_transpose=not (d in COUNTED_ROWS and n == 0),
                         start=(n == 0),
                         stop=(n == len(summands) - 1),
                     )
-            half = slice((g % 2) * ROWS, (g % 2 + 1) * ROWS)
-            nc.scalar.copy(out=new_sb[:, half, :], in_=new_ps[:])
-            if alone:
-                nc.sync.dma_start(out=out_1[t * P : (t + 1) * P, g * ROWS : (g + 1) * ROWS, :], in_=new_sb[:, half, :])
-            elif g % 2 == 1:
-                nc.sync.dma_start(out=out_1[t * P : (t + 1) * P, (g - 1) * ROWS : (g + 1) * ROWS, :], in_=new_sb[:])
+            nc.scalar.copy(out=new_sb, in_=new_ps[:])
 
         ctx.enter_context(tc.manual_schedule())
+        turn_biases()
         turn_h(0)
         group_h(0)
         quantise_h(0)
-        turn_biases()
         gate_matmuls(0, (PUSH, POP, KEEP))
         biased(0)
         turn_h(1)
@@ -436,7 +455,7 @@ def tile_stackrnn_pb_kernel(
                 if t > 0 and j == (1 if last else 4):
                     out_matmuls(t)
                 if last and j == STEPS - 1:
-                    back(t, GROUPS - 1, alone=True)
+                    back(t, GROUPS - 1, parts=1)
                 if j >= 2:
                     back(t, j - 2)
 
@@ -454,5 +473,6 @@ def tile_stackrnn_pb_kernel(
                     gate_matmuls(B_TILES - 1)
                     biased(B_TILES - 1)
                     squashed(B_TILES - 1)
-        for g in range(STEPS - 2, GROUPS - 1):
-            back(B_TILES - 1, g, alone=True)
+        for g in range(STEPS - 2, GROUPS - 2):
+            back(B_TILES - 1, g, parts=1)
+        back(B_TILES - 1, GROUPS - 2, parts=2)

@@ -31,6 +31,7 @@ BANK_ROWS = 2 * ROWS
 BANKS = DEPTH // BANK_ROWS
 POOL_BANK = BANKS - 1
 STEPS = GROUPS - 2
+SUM_BANK = 2
 COUNTED_ROWS = (0, 4 * ROWS, 6 * ROWS)
 AHEAD = 3
 
@@ -116,32 +117,29 @@ def tile_stackrnn_pb_kernel(
         turned_h, grouped_h = {}, {}
         codes_of = {}
         logits_of = {}
-        sums_of, out_of = {}, {}
+        out_of = {}
 
         def turn_h(t):
             h_words = h_of[t][:].bitcast(F32)
-            if t == 0:
-                turned_h[t] = []
-                for g in range(PASSES):
-                    hT = psum.tile([P, 2, P], F32, name="hT", tag="new_ps", bufs=3)
-                    turned_h[t].append(hT[:])
-            else:
-                hT = psum.tile([P, PASSES, 2, P], F32, name="hT", tag="new_ps", bufs=3)
-                turned_h[t] = [hT[:, g, :, :] for g in range(PASSES)]
-            for g in range(PASSES):
-                for u in range(2):
-                    words = h_words[:, 256 * g + u : 256 * (g + 1) : 2]
-                    nc.tensor.transpose(turned_h[t][g][:, u, :], words, ident_f32[:])
-            if t > 0:
-                turned_h[t] = hT
+            passes = 1 if t == 0 else PASSES
+            turned_h[t] = []
+            for first in range(0, PASSES, passes):
+                hT = psum.tile([P, passes, 2, P], F32, name="hT", tag="new_ps", bufs=3)
+                for i in range(passes):
+                    for u in range(2):
+                        g = first + i
+                        nc.tensor.transpose(hT[:, i, u, :], h_words[:, 256 * g + u : 256 * (g + 1) : 2], ident_f32[:])
+                turned_h[t].append(hT)
 
         def group_h(t):
             grouped = quant.tile([P, PASSES, P, 4], BF16, name="grouped", align_bytes=64)
-            if t == 0:
-                for g, copy in enumerate((nc.scalar.copy, nc.vector.tensor_copy)):
-                    copy(out=grouped[:, g, :, :].bitcast(F32), in_=turned_h[t][g].rearrange("p u b -> p b u"))
-            else:
-                nc.scalar.copy(out=grouped[:].bitcast(F32), in_=turned_h[t][:].rearrange("p g u b -> p g b u"))
+            passes = PASSES // len(turned_h[t])
+            for n, hT in enumerate(turned_h[t]):
+                copy = nc.scalar.copy if n == 0 else nc.vector.tensor_copy
+                copy(
+                    out=grouped[:, n * passes : (n + 1) * passes, :, :].bitcast(F32),
+                    in_=hT[:].rearrange("p g u b -> p g b u"),
+                )
             grouped_h[t] = grouped
 
         def quantise_h(t):
@@ -314,6 +312,19 @@ def tile_stackrnn_pb_kernel(
                 op=ALU.mult,
             )
 
+        summed = set()
+
+        def add_up(t, bank):
+            first, end = bank * BANK_ROWS, (bank + 1) * BANK_ROWS
+            kept = terms_of[t][:, KEEP, first:end, :]
+            for other in (
+                terms_of[t][:, PUSH, first - 1 : end - 1, :],
+                terms_of[t][:, POP, first + 1 : end + 1, :],
+            ):
+                nc.vector.tensor_tensor(out=kept, in0=kept, in1=other, op=ALU.add)
+            for d in range(first, end):
+                summed.add((t, d))
+
         def back(t, g, parts=0):
             if (t, g // 2) not in staged:
                 staged[t, g // 2] = stage.tile([P, 2 * ROWS, S], F32, name="new_sb")
@@ -335,7 +346,7 @@ def tile_stackrnn_pb_kernel(
                 d = first + i
                 pushed = edges[:, 0, :] if d == 0 else terms[:, PUSH, d - 1, :]
                 popped = edges[:, 1, :] if d == DEPTH - 1 else terms[:, POP, d + 1, :]
-                summands = (pushed, terms[:, KEEP, d, :], popped)
+                summands = (terms[:, KEEP, d, :],) if (t, d) in summed else (pushed, terms[:, KEEP, d, :], popped)
                 for n, term in enumerate(summands):
                     nc.tensor.matmul(
                         out=new_ps[:, i, :],
@@ -348,9 +359,9 @@ def tile_stackrnn_pb_kernel(
             nc.scalar.copy(out=new_sb, in_=new_ps[:])
 
         ctx.enter_context(tc.manual_schedule())
-        turn_biases()
         turn_h(0)
         group_h(0)
+        turn_biases()
         quantise_h(0)
         gate_matmuls(0, (PUSH, POP, KEEP))
         biased(0)
@@ -395,11 +406,7 @@ def tile_stackrnn_pb_kernel(
                     forward(t, 2)
                 if not last and j in (2, 4, 5):
                     forward(t + 1, {2: POOL_BANK, 4: 0, 5: 1}[j])
-                if last and j == STEPS - 1:
-                    multiply_vector(t, j * ROWS, ROWS // 2)
-                    multiply_vector(t, j * ROWS + ROWS // 2, ROWS // 2)
-                else:
-                    multiply_vector(t, j * ROWS, ROWS)
+                multiply_vector(t, j * ROWS, ROWS)
 
                 if j == 0:
                     multiply_pool(t, POP)
@@ -473,6 +480,7 @@ def tile_stackrnn_pb_kernel(
                     gate_matmuls(B_TILES - 1)
                     biased(B_TILES - 1)
                     squashed(B_TILES - 1)
-        for g in range(STEPS - 2, GROUPS - 2):
-            back(B_TILES - 1, g, parts=1)
-        back(B_TILES - 1, GROUPS - 2, parts=2)
+        add_up(B_TILES - 1, SUM_BANK)
+        back(B_TILES - 1, GROUPS - 2, parts=1)
+        back(B_TILES - 1, 2 * SUM_BANK, parts=1)
+        back(B_TILES - 1, 2 * SUM_BANK + 1, parts=2)

from contextlib import ExitStack

import concourse.mybir as mybir
from concourse.masks import make_identity

F32 = mybir.dt.float32
BF16 = mybir.dt.bfloat16
I32 = mybir.dt.int32
U32 = mybir.dt.uint32
U8 = mybir.dt.uint8
FP8X4 = mybir.dt.float8_e4m3fn_x4
FUNC = mybir.ActivationFunctionType
ALU = mybir.AluOpType

P = 128
BATCH = 1024
K = 1024
K_PASS = 512
PASSES = K // K_PASS
S = 128
DEPTH = 32
N_OUT = 512
N_GATES = 4 * S
B_TILES = BATCH // P
PUSH, POP, KEEP, TOP = 0, 1, 2, 3
BATCHES = ((0,), (1,), (2, 3), (4, 5), (6, 7))
BATCH_OF = {t: batch for batch in BATCHES for t in batch}
ROWS = 4
GROUPS = DEPTH // ROWS
BANK_ROWS = 2 * ROWS
BANKS = DEPTH // BANK_ROWS
POOL_BANK = BANKS - 1
STEPS = GROUPS - 2
SUM_BANK = 2
COUNTED_ROWS = (0, 4 * ROWS, 6 * ROWS)
AHEAD = 3

FLOPS = 2 * BATCH * K * (N_GATES + N_OUT)


def tile_stackrnn_pb_kernel(
    tc, h, stack, Wa_words, Wa_scales, ba, Ws_words, Ws_scales, bs, Wo_words, Wo_scales, bo, out_0, out_1
):
    nc = tc.nc
    with ExitStack() as ctx:
        const = ctx.enter_context(tc.tile_pool(name="const", bufs=1))
        loads = ctx.enter_context(tc.tile_pool(name="loads", bufs=AHEAD + 1))
        quant = ctx.enter_context(tc.tile_pool(name="quant", bufs=3))
        soft = ctx.enter_context(tc.tile_pool(name="soft", bufs=1))
        gate_pool = ctx.enter_context(tc.tile_pool(name="gates", bufs=2))
        term_pool = ctx.enter_context(tc.tile_pool(name="terms", bufs=2))
        stage = ctx.enter_context(tc.tile_pool(name="stage", bufs=4))
        psum = ctx.enter_context(tc.psum_pool(name="psum", bufs=1))

        h_of, x_of = {}, {}

        def load_h(t, queue):
            h_of[t] = loads.tile([P, K], BF16, name="h_sb", bufs=5)
            queue.dma_start(out=h_of[t][:], in_=h[t * P : (t + 1) * P, :])

        def load_x(t):
            x_of[t] = loads.tile([P, DEPTH, S], BF16, name="x_sb")
            nc.sync.dma_start(out=x_of[t][:], in_=stack[t * P : (t + 1) * P, :, :])

        bias_rows = const.tile([P, P], BF16, name="bias_rows")
        nc.vector.memset(bias_rows[:].bitcast(I32), 0)
        w_codes = const.tile([P, PASSES, N_GATES + N_OUT], U32, name="w_codes", align_bytes=64)
        w_scales = const.tile([P, PASSES, N_GATES + N_OUT], U8, name="w_scales", align_bytes=64)
        nc.vector.memset(w_scales[:].bitcast(I32), 0)

        load_h(0, nc.scalar)
        nc.scalar.dma_start(out=bias_rows[0:3, :], in_=ba.rearrange("(a s) -> a s", a=3))
        nc.scalar.dma_start(out=bias_rows[3:4, :], in_=bs.rearrange("(a s) -> a s", a=1))

        ident_f32 = const.tile([P, P], F32, name="ident_f32")
        make_identity(nc, ident_f32[:])
        ident_bf16 = const.tile([P, P], BF16, name="ident_bf16")
        make_identity(nc, ident_bf16[:])
        warm = const.tile([P, 1], F32, name="warm")
        nc.scalar.activation(out=warm[:], in_=ident_f32[:, 0:1], func=FUNC.Exp)

        def load_weights(words, scales, first, width):
            for quad in range(4):
                nc.sync.dma_start(
                    out=w_scales[32 * quad : 32 * quad + 4, :, first : first + width].bitcast(I32),
                    in_=scales[:, 4 * quad : 4 * quad + 4, :].rearrange("g r n -> r g n").bitcast(I32),
                )
            nc.sync.dma_start(
                out=w_codes[:, :, first : first + width].bitcast(I32),
                in_=words.rearrange("g p n t -> p g (n t)").bitcast(I32),
            )

        load_weights(Wa_words, Wa_scales, 0, 3 * S)
        load_h(1, nc.sync)
        load_h(2, nc.sync)
        load_x(0)
        load_weights(Ws_words, Ws_scales, 3 * S, S)
        load_h(3, nc.sync)
        load_h(4, nc.sync)
        load_x(1)
        for t in range(5, B_TILES):
            load_h(t, nc.sync)
        load_weights(Wo_words, Wo_scales, N_GATES, N_OUT)
        bo_all = const.tile([P, N_OUT], BF16, name="bo_all")
        nc.sync.dma_start(out=bo_all[:], in_=bo.partition_broadcast(P))
        for t in range(2, AHEAD):
            load_x(t)
        bias_col = const.tile([P, 4], F32, name="bias_col")
        half_bs = const.tile([P, 1], F32, name="half_bs")

        def turn_biases():
            bias_ps = psum.tile([P, P], BF16, name="bias_ps", tag="bank_a")
            nc.tensor.transpose(bias_ps[:], bias_rows[:], ident_bf16[:])
            nc.vector.tensor_copy(out=bias_col[:], in_=bias_ps[:, 0:4])
            nc.vector.tensor_scalar_mul(out=half_bs[:], in0=bias_col[:, 3:4], scalar1=0.5)

        turned_h, grouped_h = {}, {}
        codes_of = {}
        logits_of = {}
        out_of = {}

        def turn_h(t):
            h_words = h_of[t][:].bitcast(F32)
            passes = 1 if t == 0 else PASSES
            turned_h[t] = []
            for first in range(0, PASSES, passes):
                hT = psum.tile([P, passes, 2, P], F32, name="hT", tag="new_ps", bufs=3)
                for i in range(passes):
                    for u in range(2):
                        g = first + i
                        nc.tensor.transpose(hT[:, i, u, :], h_words[:, 256 * g + u : 256 * (g + 1) : 2], ident_f32[:])
                turned_h[t].append(hT)

        def group_h(t):
            grouped = quant.tile([P, PASSES, P, 4], BF16, name="grouped", align_bytes=64)
            passes = PASSES // len(turned_h[t])
            for n, hT in enumerate(turned_h[t]):
                copy = nc.scalar.copy if n == 0 else nc.vector.tensor_copy
                copy(
                    out=grouped[:, n * passes : (n + 1) * passes, :, :].bitcast(F32),
                    in_=hT[:].rearrange("p g u b -> p g b u"),
                )
            grouped_h[t] = grouped

        def quantise_h(t):
            h_codes = quant.tile([P, PASSES, P], U32, name="h_codes", align_bytes=64, bufs=B_TILES)
            h_scales = quant.tile([P, PASSES, P], U8, name="h_scales", align_bytes=64, bufs=B_TILES)
            nc.vector.quantize_mx(
                out=h_codes[:].rearrange("p g b -> p (g b)").bitcast(FP8X4),
                scales=h_scales[:].rearrange("p g b -> p (g b)"),
                in_=grouped_h[t][:].rearrange("p g b t -> p (g b t)"),
            )
            codes_of[t] = (h_codes, h_scales)

        def gate_matmuls(t, gates=(PUSH, POP, KEEP, TOP)):
            h_codes, h_scales = codes_of[t]
            if t not in logits_of:
                logits_of[t] = psum.tile([P, 4, P], F32, name="logits", tag="bank_a" if t == 0 else "bank_b")
            for j in gates:
                cols = slice(j * S, (j + 1) * S)
                for g in range(PASSES):
                    nc.tensor.matmul_mx(
                        out=logits_of[t][:, j, :],
                        lhsT=w_codes[:, g, cols].bitcast(FP8X4),
                        lhsT_scale=w_scales[:, g, cols],
                        rhs=h_codes[:, g, :].bitcast(FP8X4),
                        rhs_scale=h_scales[:, g, :],
                        start=(g == 0),
                        stop=(g == PASSES - 1),
                    )

        def out_matmuls(t):
            h_codes, h_scales = codes_of[t]
            out_ps = psum.tile([P, N_OUT], F32, name="out_ps", tag="bank_a")
            for g in range(PASSES):
                nc.tensor.matmul_mx(
                    out=out_ps[:],
                    lhsT=h_codes[:, g, :].bitcast(FP8X4),
                    lhsT_scale=h_scales[:, g, :],
                    rhs=w_codes[:, g, N_GATES:].bitcast(FP8X4),
                    rhs_scale=w_scales[:, g, N_GATES:],
                    start=(g == 0),
                    stop=(g == PASSES - 1),
                )
            out_sb = stage.tile([P, N_OUT], F32, name="out_sb", bufs=2)
            nc.scalar.copy(out=out_sb[:], in_=out_ps[:])
            out_of[t] = out_sb

        def store_out(t):
            out_sb = out_of[t]
            nc.gpsimd.tensor_tensor(out=out_sb[:], in0=out_sb[:], in1=bo_all[:], op=ALU.add)
            nc.sync.dma_start(out=out_0[t * P : (t + 1) * P, :], in_=out_sb[:])

        logit_sb, tanh_half, top, peak, shifted, expo, total, inverse = {}, {}, {}, {}, {}, {}, {}, {}
        gates_of, edges_of, edge_tile, gate_tile = {}, {}, {}, {}

        def over_actions(tile, n):
            return tile[:].unsqueeze(2).to_broadcast([P, n, 3, P])

        def biased(t):
            batch = BATCH_OF[t]
            n, i = len(batch), batch.index(t)
            if i == 0:
                logit_sb[batch] = soft.tile([P, n, 3, P], F32, name="logit_sb", bufs=4)
                tanh_half[batch] = soft.tile([P, n, P], F32, name="tanh_half", bufs=4)
            for a in range(3):
                nc.scalar.activation(
                    out=logit_sb[batch][:, i, a, :],
                    in_=logits_of[t][:, a, :],
                    func=FUNC.Identity,
                    bias=bias_col[:, a : a + 1],
                )

        def squashed(t):
            batch = BATCH_OF[t]
            nc.scalar.activation(
                out=tanh_half[batch][:, batch.index(t), :],
                in_=logits_of[t][:, TOP, :],
                func=FUNC.Tanh,
                bias=half_bs[:],
                scale=0.5,
            )

        def peak_of(batch):
            n = len(batch)
            peak[batch] = soft.tile([P, n, P], F32, name="peak")
            nc.vector.tensor_reduce(
                out=peak[batch][:],
                in_=logit_sb[batch][:].rearrange("p n a b -> p n b a"),
                axis=mybir.AxisListType.X,
                op=ALU.max,
            )

        def shift(batch, engine):
            n = len(batch)
            shifted[batch] = soft.tile([P, n, 3, P], F32, name="shifted")
            engine.tensor_tensor(
                out=shifted[batch][:], in0=logit_sb[batch][:], in1=over_actions(peak[batch], n), op=ALU.subtract
            )

        def exponentials(batch):
            n = len(batch)
            expo[batch] = soft.tile([P, n, 3, P], F32, name="expo", bufs=2)
            nc.scalar.activation(out=expo[batch][:], in_=shifted[batch][:], func=FUNC.Exp)

        def top_row(batch):
            n = len(batch)
            top[batch] = soft.tile([P, n, P], F32, name="top", bufs=2)
            nc.scalar.activation(out=top[batch][:], in_=tanh_half[batch][:], func=FUNC.Copy, bias=0.5, scale=0.5)

        def total_of(batch, engine):
            n = len(batch)
            total01 = soft.tile([P, n, P], F32, name="total01")
            engine.tensor_tensor(out=total01[:], in0=expo[batch][:, :, 0, :], in1=expo[batch][:, :, 1, :], op=ALU.add)
            total[batch] = soft.tile([P, n, P], F32, name="total")
            engine.tensor_tensor(out=total[batch][:], in0=total01[:], in1=expo[batch][:, :, 2, :], op=ALU.add)

        def invert(batch):
            n = len(batch)
            inverse[batch] = soft.tile([P, n, P], F32, name="inverse")
            nc.vector.reciprocal(out=inverse[batch][:], in_=total[batch][:])

        def normalise(batch, engine):
            n = len(batch)
            gates = gate_pool.tile([P, n, 3, P], F32, name="gates")
            engine.tensor_tensor(out=gates[:], in0=expo[batch][:], in1=over_actions(inverse[batch], n), op=ALU.mult)
            edges = gate_pool.tile([P, n, 2, P], F32, name="edges")
            gate_tile[batch], edge_tile[batch] = gates, edges
            for i, t in enumerate(batch):
                gates_of[t] = gates[:, i, :, :]
                edges_of[t] = edges[:, i, :, :]

        def push_edge(batch):
            nc.gpsimd.tensor_tensor(
                out=edge_tile[batch][:, :, 0, :], in0=gate_tile[batch][:, :, PUSH, :], in1=top[batch][:], op=ALU.mult
            )

        def pop_edge(batch):
            nc.scalar.mul(out=edge_tile[batch][:, :, 1, :], in_=gate_tile[batch][:, :, POP, :], mul=-1.0)

        turned = {}
        terms_of = {}
        staged = {}

        def forward(t, bank):
            xT = psum.tile([P, BANK_ROWS, P], BF16, name="xT", tag="xT", bufs=3)
            for i in range(BANK_ROWS):
                nc.tensor.transpose(xT[:, i, :], x_of[t][:, bank * BANK_ROWS + i, :], ident_bf16[:])
            turned[t, bank] = xT
            if bank == POOL_BANK:
                xT_sb = stage.tile([P, BANK_ROWS, P], BF16, name="xT_sb", bufs=2)
                nc.scalar.copy(out=xT_sb[:], in_=xT[:])
                turned[t, bank] = xT_sb

        def multiply_vector(t, first_row, rows):
            bank, first = divmod(first_row, BANK_ROWS)
            shape = [P, 3, rows, P]
            nc.vector.tensor_tensor(
                out=terms_of[t][:, :, first_row : first_row + rows, :],
                in0=turned[t, bank][:, first : first + rows, :].unsqueeze(1).to_broadcast(shape),
                in1=gates_of[t].unsqueeze(2).to_broadcast(shape),
                op=ALU.mult,
            )

        def multiply_pool(t, a):
            rows = BANK_ROWS - 1 if a == PUSH else BANK_ROWS
            first = POOL_BANK * BANK_ROWS
            nc.gpsimd.tensor_tensor(
                out=terms_of[t][:, a, first : first + rows, :],
                in0=turned[t, POOL_BANK][:, 0:rows, :],
                in1=gates_of[t][:, a, :].unsqueeze(1).to_broadcast([P, rows, P]),
                op=ALU.mult,
            )

        summed = set()

        def add_up(t, bank):
            first, end = bank * BANK_ROWS, (bank + 1) * BANK_ROWS
            kept = terms_of[t][:, KEEP, first:end, :]
            for other in (
                terms_of[t][:, PUSH, first - 1 : end - 1, :],
                terms_of[t][:, POP, first + 1 : end + 1, :],
            ):
                nc.vector.tensor_tensor(out=kept, in0=kept, in1=other, op=ALU.add)
            for d in range(first, end):
                summed.add((t, d))

        def back(t, g, parts=0):
            if (t, g // 2) not in staged:
                staged[t, g // 2] = stage.tile([P, 2 * ROWS, S], F32, name="new_sb")
            new_sb = staged[t, g // 2]
            rows = ROWS // max(parts, 1)
            for first in range(0, ROWS, rows):
                at = slice((g % 2) * ROWS + first, (g % 2) * ROWS + first + rows)
                add_rows(t, g * ROWS + first, rows, new_sb[:, at, :])
                if parts:
                    d = g * ROWS + first
                    nc.sync.dma_start(out=out_1[t * P : (t + 1) * P, d : d + rows, :], in_=new_sb[:, at, :])
            if g % 2 == 1 and not parts:
                nc.sync.dma_start(out=out_1[t * P : (t + 1) * P, (g - 1) * ROWS : (g + 1) * ROWS, :], in_=new_sb[:])

        def add_rows(t, first, rows, new_sb):
            terms, edges = terms_of[t], edges_of[t]
            new_ps = psum.tile([P, rows, S], F32, name="new_ps", tag="new_ps", bufs=3)
            for i in range(rows):
                d = first + i
                pushed = edges[:, 0, :] if d == 0 else terms[:, PUSH, d - 1, :]
                popped = edges[:, 1, :] if d == DEPTH - 1 else terms[:, POP, d + 1, :]
                summands = (terms[:, KEEP, d, :],) if (t, d) in summed else (pushed, terms[:, KEEP, d, :], popped)
                for n, term in enumerate(summands):
                    nc.tensor.matmul(
                        out=new_ps[:, i, :],
                        lhsT=term,
                        rhs=ident_f32[:],
                        is_transpose=not (d in COUNTED_ROWS and n == 0),
                        start=(n == 0),
                        stop=(n == len(summands) - 1),
                    )
            nc.scalar.copy(out=new_sb, in_=new_ps[:])

        ctx.enter_context(tc.manual_schedule())
        turn_h(0)
        group_h(0)
        turn_biases()
        quantise_h(0)
        gate_matmuls(0, (PUSH, POP, KEEP))
        biased(0)
        turn_h(1)
        group_h(1)
        peak_of((0,))
        shift((0,), nc.vector)
        exponentials((0,))
        quantise_h(1)
        turn_h(2)
        gate_matmuls(1, (PUSH, POP, KEEP))
        biased(1)
        forward(0, 0)
        forward(0, POOL_BANK)
        total_of((0,), nc.vector)
        invert((0,))
        normalise((0,), nc.vector)
        peak_of((1,))
        shift((1,), nc.gpsimd)
        gate_matmuls(0, (TOP,))
        squashed(0)
        top_row((0,))
        group_h(2)
        gate_matmuls(1, (TOP,))
        forward(0, 1)
        turn_h(3)
        push_edge((0,))
        pop_edge((0,))
        squashed(1)
        exponentials((1,))
        top_row((1,))

        for t in range(B_TILES):
            last = t + 1 == B_TILES
            begun = {0: (2, 3), 2: (4, 5), 4: (6, 7)}.get(t)
            finished = {0: (1,), 1: (2, 3), 3: (4, 5), 5: (6, 7)}.get(t)
            if t + AHEAD < B_TILES:
                load_x(t + AHEAD)
            terms_of[t] = term_pool.tile([P, 3, DEPTH, P], F32, name="terms")
            for j in range(STEPS):
                if j == 1:
                    forward(t, 2)
                if not last and j in (2, 4, 5):
                    forward(t + 1, {2: POOL_BANK, 4: 0, 5: 1}[j])
                multiply_vector(t, j * ROWS, ROWS)

                if j == 0:
                    multiply_pool(t, POP)
                    if t in (3, 5):
                        total_of(finished, nc.gpsimd)
                if j == 1:
                    if t in (0, 1):
                        total_of(finished, nc.gpsimd)
                    if t in (2, 4):
                        shift(begun, nc.gpsimd)
                    if t > 1:
                        store_out(t - 1)
                if j == 2:
                    multiply_pool(t, KEEP)
                if j == 3 and t in (0, 1):
                    normalise(finished, nc.gpsimd)
                if j == 4:
                    if t == 1:
                        store_out(0)
                    if t in (3, 5):
                        normalise(finished, nc.gpsimd)
                    multiply_pool(t, PUSH)
                if j == 5:
                    if finished is not None:
                        push_edge(finished)
                    if t == 0:
                        shift(begun, nc.gpsimd)
                    if last:
                        store_out(t)

                if t == 1 and j == 0:
                    exponentials(finished)
                    top_row(finished)
                if t > 0 and j == 0:
                    back(t - 1, 4)
                    back(t - 1, 5)
                if t > 0 and j == 1:
                    back(t - 1, 6)
                    back(t - 1, 7)

                if begun is not None and j == (3 if t == 0 else 0):
                    peak_of(begun)
                if finished is not None and j == (2 if t < 2 else 3):
                    invert(finished)
                if finished is not None and j == (4 if t == 0 else 5):
                    pop_edge(finished)
                if t in (2, 4) and j == 5:
                    exponentials(begun)
                    top_row(begun)

                if t == 1 and j == 1:
                    out_matmuls(0)
                if t > 0 and j == (1 if last else 4):
                    out_matmuls(t)
                if last and j == STEPS - 1:
                    back(t, GROUPS - 1, parts=1)
                if j >= 2:
                    back(t, j - 2)

                if t == 0:
                    if j + 3 < B_TILES:
                        group_h(j + 3)
                    if j > 0:
                        gate_matmuls(j + 1)
                        biased(j + 1)
                        squashed(j + 1)
                    if j + 4 < B_TILES:
                        turn_h(j + 4)
                    quantise_h(j + 2)
                if t == 1 and j == 0:
                    gate_matmuls(B_TILES - 1)
                    biased(B_TILES - 1)
                    squashed(B_TILES - 1)
        add_up(B_TILES - 1, SUM_BANK)
        back(B_TILES - 1, GROUPS - 2, parts=1)
        back(B_TILES - 1, 2 * SUM_BANK, parts=1)
        back(B_TILES - 1, 2 * SUM_BANK + 1, parts=2)
